import numpy as np
import ml_dtypes


def mxq(x, axis, fmt="e4m3"):
    dtype, down = {"e4m3": (ml_dtypes.float8_e4m3fn, 7), "e5m2": (ml_dtypes.float8_e5m2, 14)}[fmt]
    v = np.moveaxis(np.asarray(x, np.float32).astype(ml_dtypes.bfloat16).astype(np.float64), axis, -1)
    blocks = v.reshape(v.shape[:-1] + (-1, 32))
    amax = np.abs(blocks).max(-1, keepdims=True)
    byte = np.maximum(np.where(amax > 0, np.frexp(amax)[1] - 1 + 127, 0) - down, 1)
    scale = np.exp2(byte - 127.0)
    codes = (blocks / scale).astype(np.float32).astype(dtype).astype(np.float64)
    return np.moveaxis((codes * scale).reshape(v.shape), -1, axis)


WIDE = False


def mx_kscale(k):
    if not WIDE:
        return np.ones(k)
    levels = np.array([20, -20, 10, -10, 0])
    a = np.random.permutation(np.resize(levels, k // 512 * 4)).reshape(k // 512, 4)
    idx = np.arange(k)
    return np.exp2(a[idx // 512, idx % 128 // 32])


BF16 = ml_dtypes.bfloat16


def bf(x):
    return np.asarray(x, np.float32).astype(BF16)


def f64(x):
    return np.asarray(x).astype(np.float64)


B, H, W, FI, FO = 2, 32, 64, 1024, 512

OFFSETS = [(-1, 0), (1, 0), (0, -1), (0, 1), (-1, -1), (-1, 1), (1, -1), (1, 1)]


def nsum(Z, H, W):
    Bn, N, F = Z.shape
    P = np.pad(Z.reshape(Bn, H, W, F), ((0, 0), (1, 1), (1, 1), (0, 0)))
    S = np.zeros((Bn, H, W, F))
    for dr, dc in OFFSETS:
        S = S + P[:, 1 + dr:1 + dr + H, 1 + dc:1 + dc + W, :]
    return S.reshape(Bn, N, F)


def setup_inputs():
    u = mx_kscale(FO)
    X = np.random.standard_normal((B, H * W, FI)) * 0.5
    Wm = np.random.standard_normal((FI, FO)) / np.sqrt(FI) / u
    b = np.random.standard_normal(FO) * 0.2
    g = np.random.standard_normal((B, H * W, FO)) * np.exp2(np.random.randint(-12, 1, (B, H * W, 1))) * 4.0 * u
    return {"X": bf(X), "Wm": bf(Wm), "b": bf(b), "H": H, "W": W, "grad_out": bf(g)}


def reference(X, Wm, b, H, W, grad_out):
    G = mxq(f64(grad_out), 2, "e5m2") @ mxq(f64(Wm), 1, "e4m3").T
    return nsum(G, H, W)

@@ -1,0 +1,226 @@
+from contextlib import ExitStack
+
+import concourse.mybir as mybir
+from concourse.masks import make_identity
+
+F32 = mybir.dt.float32
+BF16 = mybir.dt.bfloat16
+U32 = mybir.dt.uint32
+U8 = mybir.dt.uint8
+E5X4 = mybir.dt.float8_e5m2_x4
+E4X4 = mybir.dt.float8_e4m3fn_x4
+ADD = mybir.AluOpType.add
+MULT = mybir.AluOpType.mult
+
+P = 128
+NODES = 4096
+K = 512
+FEAT = 1024
+NT = 32
+XS = 32
+GRP = 4
+FLOPS = 2 * NODES * K * FEAT
+BYTES = NODES * K * 2 + FEAT * K * 2 + NODES * FEAT * 4
+
+SHIFTS = (-1, 0, 1)
+
+
+def is_direct(t, fh):
+    return t % 2 == 1 and fh == 1
+
+
+def tile_graphconvlayer_t_kernel(tc, X, Wm, b, H, W, grad_out, out):
+    nc = tc.nc
+    assert H == 32 and W == 64
+    g_flat = grad_out.flatten_outer_dims()
+    g_pt = g_flat.rearrange("(p t) k -> p t k", t=NT)
+    g_mc = g_flat.rearrange("(m c) k -> m c k", c=64)
+    w_pj = Wm.rearrange("(j p) k -> p j k", p=P)
+    out_pt = out.flatten_outer_dims().rearrange("(p t) f -> p t f", t=NT)
+
+    with ExitStack() as ctx:
+        keep = ctx.enter_context(tc.tile_pool(name="keep", bufs=1))
+        work = ctx.enter_context(tc.tile_pool(name="work", bufs=2))
+        psum = ctx.enter_context(tc.psum_pool(name="psum", bufs=2))
+
+        w_sb = keep.tile([P, 8 * K], BF16, name="w_sb")
+        gx_sb = keep.tile([P, K], BF16, name="gx_sb")
+        g_sb = [keep.tile([P, GRP * K], BF16, name="g_sb%d" % g) for g in range(NT // GRP)]
+
+        def load_w(h):
+            nc.sync.dma_start(
+                out=w_sb[:, h * 4 * K:(h + 1) * 4 * K].rearrange("p (j k) -> p j k", k=K),
+                in_=w_pj[:, h * 4:(h + 1) * 4, :],
+            )
+
+        def load_g(g):
+            nc.sync.dma_start(
+                out=g_sb[g][:].rearrange("p (t k) -> p t k", k=K),
+                in_=g_pt[:, g * GRP:(g + 1) * GRP, :],
+            )
+
+        load_w(0)
+        nc.sync.dma_start(out=gx_sb[0:P:2, :], in_=g_mc[:, 32, :])
+        nc.sync.dma_start(out=gx_sb[1:P:2, :], in_=g_mc[:, 31, :])
+        load_g(0)
+        load_w(1)
+        for g in range(1, NT // GRP):
+            load_g(g)
+
+        ident = keep.tile([P, P], F32, name="ident")
+        make_identity(nc, ident[:])
+        id_pairs = ident[:].rearrange("p (a e) -> p a e", e=2)
+        mask_even = keep.tile([P, 1], F32, name="mask_even")
+        mask_odd = keep.tile([P, 1], F32, name="mask_odd")
+        nc.vector.tensor_reduce(out=mask_even[:], in_=id_pairs[:, :, 0], axis=mybir.AxisListType.X, op=ADD)
+        nc.vector.tensor_reduce(out=mask_odd[:], in_=id_pairs[:, :, 1], axis=mybir.AxisListType.X, op=ADD)
+
+        grp = {}
+        for s in SHIFTS:
+            for bb in range(2):
+                grp[(s, bb)] = keep.tile([P, GRP * P * 4], BF16, name="grp%d_%d" % (s + 1, bb), align_bytes=64)
+            grp[(s, "x")] = keep.tile([P, P * 4], BF16, name="grpx%d" % (s + 1), align_bytes=64)
+        for key in (0, 1, "x"):
+            up = grp[(1, key)][:].rearrange("p (a c e) -> p a c e", c=64, e=4)
+            nc.vector.memset(up[:, :, 62:64, :], 0.0)
+            dn = grp[(-1, key)][:].rearrange("p (a c e) -> p a c e", c=64, e=4)
+            nc.vector.memset(dn[:, :, 0:2, :], 0.0)
+
+        codes = {}
+        scales = {}
+        for s in SHIFTS:
+            codes[s] = keep.tile([P, (NT + 1) * P], U32, name="codes%d" % (s + 1), align_bytes=64)
+            scales[s] = keep.tile([P, (NT + 1) * P], U8, name="scales%d" % (s + 1), align_bytes=64)
+        w_grp = keep.tile([P, FEAT * 4], BF16, name="w_grp", align_bytes=64)
+        w_codes = keep.tile([P, FEAT], U32, name="w_codes", align_bytes=64)
+        w_scales = keep.tile([P, FEAT], U8, name="w_scales", align_bytes=64)
+        cx = keep.tile([P, FEAT], F32, name="cx")
+
+        def transpose_pair(xt, src32, first, count):
+            for jj in range(count):
+                for u in range(2):
+                    lo = (first + jj) * 256 + u * P
+                    nc.tensor.transpose(xt[:, u, jj * P:(jj + 1) * P], src32[:, lo:lo + P], ident[:])
+
+        def prep_w(h):
+            w32 = w_sb[:].bitcast(F32)
+            wg32 = w_grp[:].bitcast(F32)
+            for jp in (2 * h, 2 * h + 1):
+                xt = psum.tile([P, 2, 256], F32, tag="xt", bufs=2, name="xt")
+                transpose_pair(xt, w32, 2 * jp, 2)
+                nc.vector.tensor_copy(
+                    out=wg32[:, jp * 512:(jp + 1) * 512].rearrange("p (f u) -> p f u", u=2),
+                    in_=xt[:].rearrange("p u f -> p f u"),
+                )
+            nc.vector.quantize_mx(
+                out=w_codes[:, h * 512:(h + 1) * 512].bitcast(E4X4),
+                scales=w_scales[:, h * 512:(h + 1) * 512],
+                in_=w_grp[:, h * 2048:(h + 1) * 2048],
+            )
+
+        def regroup(xt, ntile, key, word0):
+            src = xt[:, :, 0:ntile * P].rearrange("p u (a c) -> p a c u", c=64)
+            for s in SHIFTS:
+                dst = grp[(s, key)][:].bitcast(F32)[:, word0:word0 + ntile * 256].rearrange(
+                    "p (a c u) -> p a c u", c=64, u=2)
+                if s == 0:
+                    nc.scalar.copy(out=dst, in_=src)
+                elif s == 1:
+                    nc.scalar.copy(out=dst[:, :, 0:62, :], in_=src[:, :, 2:64, :])
+                else:
+                    nc.scalar.copy(out=dst[:, :, 2:64, :], in_=src[:, :, 0:62, :])
+
+        def quantise(key, slot0, ntile):
+            for s in SHIFTS:
+                nc.vector.quantize_mx(
+                    out=codes[s][:, slot0 * P:(slot0 + ntile) * P].bitcast(E5X4),
+                    scales=scales[s][:, slot0 * P:(slot0 + ntile) * P],
+                    in_=grp[(s, key)][:],
+                )
+
+        def prep_x():
+            xt = psum.tile([P, 2, 256], F32, tag="xt", bufs=2, name="xt")
+            transpose_pair(xt, gx_sb[:].bitcast(F32), 0, 1)
+            regroup(xt, 1, "x", 0)
+            quantise("x", XS, 1)
+
+        def prep_g(g):
+            g32 = g_sb[g][:].bitcast(F32)
+            for bk in range(2):
+                xt = psum.tile([P, 2, 256], F32, tag="xt", bufs=2, name="xt")
+                transpose_pair(xt, g32, 2 * bk, 2)
+                regroup(xt, 2, g % 2, bk * 512)
+            quantise(g % 2, g * GRP, GRP)
+
+        def mx(acc, s, slot, fh, start, stop):
+            nc.tensor.matmul_mx(
+                out=acc[:],
+                lhsT=codes[s][:, slot * P:(slot + 1) * P].bitcast(E5X4),
+                lhsT_scale=scales[s][:, slot * P:(slot + 1) * P],
+                rhs=w_codes[:, fh * 512:(fh + 1) * 512].bitcast(E4X4),
+                rhs_scale=w_scales[:, fh * 512:(fh + 1) * 512],
+                start=start,
+                stop=stop,
+            )
+
+        def column_sum_direct(slot, fh, dst):
+            pb = psum.tile([P, 512], F32, tag="pb", bufs=3, name="pb")
+            mx(pb, -1, slot, fh, True, False)
+            mx(pb, 0, slot, fh, False, False)
+            mx(pb, 1, slot, fh, False, True)
+            nc.scalar.copy(out=dst, in_=pb[:])
+
+        prep_w(0)
+        prep_x()
+        prep_g(0)
+        prep_w(1)
+        for fh in range(2):
+            column_sum_direct(XS, fh, cx[:, fh * 512:(fh + 1) * 512])
+
+        csum = {}
+        stage = {}
+
+        def unit(t, fh):
+            fs = slice(fh * 512, (fh + 1) * 512)
+            pa = psum.tile([P, 512], F32, tag="pa", bufs=3, name="pa")
+            mx(pa, -1, t, fh, True, False)
+            mx(pa, 1, t, fh, False, True)
+            d_dst = stage[t // 2][:, t % 2, fs]
+            if is_direct(t, fh):
+                column_sum_direct(t, fh, csum[t][:, fs])
+                bsb = None
+            else:
+                pb = psum.tile([P, 512], F32, tag="pb", bufs=3, name="pb")
+                mx(pb, 0, t, fh, True, True)
+                bsb = work.tile([P, 512], F32, tag="bsb", bufs=4, name="bsb")
+                nc.scalar.copy(out=bsb[:], in_=pb[:])
+            if t == 0:
+                nc.vector.scalar_tensor_tensor(
+                    out=d_dst, in0=cx[:, fs], scalar=mask_odd[:, 0:1], in1=pa[:], op0=MULT, op1=ADD)
+            else:
+                nc.vector.tensor_tensor(out=d_dst, in0=pa[:], in1=csum[t - 1][:, fs], op=ADD)
+            if bsb is not None:
+                nc.vector.tensor_tensor(out=csum[t][:, fs], in0=pa[:], in1=bsb[:], op=ADD)
+
+        def finish(t):
+            dst = stage[t // 2][:, t % 2, :]
+            if t == NT - 1:
+                nc.vector.scalar_tensor_tensor(
+                    out=dst, in0=cx[:], scalar=mask_even[:, 0:1], in1=dst, op0=MULT, op1=ADD)
+            else:
+                nc.gpsimd.tensor_tensor(out=dst, in0=dst, in1=csum[t + 1][:], op=ADD)
+            if t % 2 == 1:
+                nc.sync.dma_start(out=out_pt[:, t - 1:t + 1, :], in_=stage[t // 2][:])
+
+        for g in range(NT // GRP):
+            if g + 1 < NT // GRP:
+                prep_g(g + 1)
+            for t in range(g * GRP, (g + 1) * GRP):
+                csum[t] = work.tile([P, FEAT], F32, tag="csum", bufs=5, name="csum")
+                if t % 2 == 0:
+                    stage[t // 2] = work.tile([P, 2, FEAT], F32, tag="stage", bufs=4, name="stage")
+                for fh in range(2):
+                    unit(t, fh)
+                if t >= 1:
+                    finish(t - 1)
+        finish(NT - 1)

@@ -26,7 +26,14 @@ SHIFTS = (-1, 0, 1)
 
 
 def is_direct(t, fh):
-    return t % 2 == 1 and fh == 1
+    return fh == 1 and t % 4 != 0
+
+
+def on_vector(t):
+    return t % 4 == 3 or t >= NT - 2
+
+
+GROUPS = ((0, 2), (2, 2), (4, 4), (8, 4), (12, 4), (16, 4), (20, 4), (24, 4), (28, 4))
 
 
 def tile_graphconvlayer_t_kernel(tc, X, Wm, b, H, W, grad_out, out):
@@ -45,7 +52,7 @@ def tile_graphconvlayer_t_kernel(tc, X, Wm, b, H, W, grad_out, out):
 
         w_sb = keep.tile([P, 8 * K], BF16, name="w_sb")
         gx_sb = keep.tile([P, K], BF16, name="gx_sb")
-        g_sb = [keep.tile([P, GRP * K], BF16, name="g_sb%d" % g) for g in range(NT // GRP)]
+        g_sb = [keep.tile([P, n * K], BF16, name="g_sb%d" % t0) for (t0, n) in GROUPS]
 
         def load_w(h):
             nc.sync.dma_start(
@@ -56,15 +63,15 @@ def tile_graphconvlayer_t_kernel(tc, X, Wm, b, H, W, grad_out, out):
         def load_g(g):
             nc.sync.dma_start(
                 out=g_sb[g][:].rearrange("p (t k) -> p t k", k=K),
-                in_=g_pt[:, g * GRP:(g + 1) * GRP, :],
+                in_=g_pt[:, GROUPS[g][0]:GROUPS[g][0] + GROUPS[g][1], :],
             )
 
         load_w(0)
+        load_g(0)
         nc.sync.dma_start(out=gx_sb[0:P:2, :], in_=g_mc[:, 32, :])
         nc.sync.dma_start(out=gx_sb[1:P:2, :], in_=g_mc[:, 31, :])
-        load_g(0)
         load_w(1)
-        for g in range(1, NT // GRP):
+        for g in range(1, len(GROUPS)):
             load_g(g)
 
         ident = keep.tile([P, P], F32, name="ident")
@@ -135,7 +142,7 @@ def tile_graphconvlayer_t_kernel(tc, X, Wm, b, H, W, grad_out, out):
                 nc.vector.quantize_mx(
                     out=codes[s][:, slot0 * P:(slot0 + ntile) * P].bitcast(E5X4),
                     scales=scales[s][:, slot0 * P:(slot0 + ntile) * P],
-                    in_=grp[(s, key)][:],
+                    in_=grp[(s, key)][:, 0:ntile * P * 4],
                 )
 
         def prep_x():
@@ -146,11 +153,11 @@ def tile_graphconvlayer_t_kernel(tc, X, Wm, b, H, W, grad_out, out):
 
         def prep_g(g):
             g32 = g_sb[g][:].bitcast(F32)
-            for bk in range(2):
+            for bk in range(GROUPS[g][1] // 2):
                 xt = psum.tile([P, 2, 256], F32, tag="xt", bufs=2, name="xt")
                 transpose_pair(xt, g32, 2 * bk, 2)
                 regroup(xt, 2, g % 2, bk * 512)
-            quantise(g % 2, g * GRP, GRP)
+            quantise(g % 2, GROUPS[g][0], GROUPS[g][1])
 
         def mx(acc, s, slot, fh, start, stop):
             nc.tensor.matmul_mx(
@@ -171,8 +178,8 @@ def tile_graphconvlayer_t_kernel(tc, X, Wm, b, H, W, grad_out, out):
             nc.scalar.copy(out=dst, in_=pb[:])
 
         prep_w(0)
-        prep_x()
         prep_g(0)
+        prep_x()
         prep_w(1)
         for fh in range(2):
             column_sum_direct(XS, fh, cx[:, fh * 512:(fh + 1) * 512])
@@ -207,20 +214,25 @@ def tile_graphconvlayer_t_kernel(tc, X, Wm, b, H, W, grad_out, out):
             if t == NT - 1:
                 nc.vector.scalar_tensor_tensor(
                     out=dst, in0=cx[:], scalar=mask_even[:, 0:1], in1=dst, op0=MULT, op1=ADD)
+            elif on_vector(t):
+                nc.vector.tensor_tensor(out=dst, in0=dst, in1=csum[t + 1][:], op=ADD)
             else:
                 nc.gpsimd.tensor_tensor(out=dst, in0=dst, in1=csum[t + 1][:], op=ADD)
-            if t % 2 == 1:
+            if t >= NT - 2:
+                nc.sync.dma_start(out=out_pt[:, t, :], in_=dst)
+            elif t % 2 == 1:
                 nc.sync.dma_start(out=out_pt[:, t - 1:t + 1, :], in_=stage[t // 2][:])
 
-        for g in range(NT // GRP):
-            if g + 1 < NT // GRP:
+        for g in range(len(GROUPS)):
+            if g + 1 < len(GROUPS):
                 prep_g(g + 1)
-            for t in range(g * GRP, (g + 1) * GRP):
+            for t in range(GROUPS[g][0], GROUPS[g][0] + GROUPS[g][1]):
                 csum[t] = work.tile([P, FEAT], F32, tag="csum", bufs=5, name="csum")
                 if t % 2 == 0:
                     stage[t // 2] = work.tile([P, 2, FEAT], F32, tag="stage", bufs=4, name="stage")
                 for fh in range(2):
                     unit(t, fh)
+                if t == NT - 1:
+                    finish(t)
                 if t >= 1:
                     finish(t - 1)
-        finish(NT - 1)

@@ -16,9 +16,12 @@ P = 128
 NODES = 4096
 K = 512
 FEAT = 1024
+HALF = 512
 NT = 32
-XS = 32
+XS = 8
 GRP = 4
+NG = NT // GRP
+RING = 8
 FLOPS = 2 * NODES * K * FEAT
 BYTES = NODES * K * 2 + FEAT * K * 2 + NODES * FEAT * 4
 
@@ -30,10 +33,7 @@ def is_direct(t, fh):
 
 
 def on_vector(t):
-    return t % 4 == 3 or t >= NT - 2
-
-
-GROUPS = ((0, 2), (2, 2), (4, 4), (8, 4), (12, 4), (16, 4), (20, 4), (24, 4), (28, 4))
+    return t % 4 == 1 or t >= NT - 2
 
 
 def tile_graphconvlayer_t_kernel(tc, X, Wm, b, H, W, grad_out, out):
@@ -47,12 +47,11 @@ def tile_graphconvlayer_t_kernel(tc, X, Wm, b, H, W, grad_out, out):
 
     with ExitStack() as ctx:
         keep = ctx.enter_context(tc.tile_pool(name="keep", bufs=1))
-        work = ctx.enter_context(tc.tile_pool(name="work", bufs=2))
         psum = ctx.enter_context(tc.psum_pool(name="psum", bufs=2))
 
         w_sb = keep.tile([P, 8 * K], BF16, name="w_sb")
         gx_sb = keep.tile([P, K], BF16, name="gx_sb")
-        g_sb = [keep.tile([P, n * K], BF16, name="g_sb%d" % t0) for (t0, n) in GROUPS]
+        g_sb = [keep.tile([P, GRP * K], BF16, name="g_sb%d" % g) for g in range(NG)]
 
         def load_w(h):
             nc.sync.dma_start(
@@ -63,101 +62,89 @@ def tile_graphconvlayer_t_kernel(tc, X, Wm, b, H, W, grad_out, out):
         def load_g(g):
             nc.sync.dma_start(
                 out=g_sb[g][:].rearrange("p (t k) -> p t k", k=K),
-                in_=g_pt[:, GROUPS[g][0]:GROUPS[g][0] + GROUPS[g][1], :],
+                in_=g_pt[:, g * GRP:(g + 1) * GRP, :],
             )
 
         load_w(0)
-        load_g(0)
         nc.sync.dma_start(out=gx_sb[0:P:2, :], in_=g_mc[:, 32, :])
         nc.sync.dma_start(out=gx_sb[1:P:2, :], in_=g_mc[:, 31, :])
+        load_g(0)
         load_w(1)
-        for g in range(1, len(GROUPS)):
+        for g in range(1, NG):
             load_g(g)
+
+        ctx.enter_context(tc.manual_schedule())
 
         ident = keep.tile([P, P], F32, name="ident")
         make_identity(nc, ident[:])
         id_pairs = ident[:].rearrange("p (a e) -> p a e", e=2)
         mask_even = keep.tile([P, 1], F32, name="mask_even")
         mask_odd = keep.tile([P, 1], F32, name="mask_odd")
-        nc.vector.tensor_reduce(out=mask_even[:], in_=id_pairs[:, :, 0], axis=mybir.AxisListType.X, op=ADD)
-        nc.vector.tensor_reduce(out=mask_odd[:], in_=id_pairs[:, :, 1], axis=mybir.AxisListType.X, op=ADD)
 
         grp = {}
         for s in SHIFTS:
             for bb in range(2):
                 grp[(s, bb)] = keep.tile([P, GRP * P * 4], BF16, name="grp%d_%d" % (s + 1, bb), align_bytes=64)
             grp[(s, "x")] = keep.tile([P, P * 4], BF16, name="grpx%d" % (s + 1), align_bytes=64)
-        for key in (0, 1, "x"):
+        for key in ("x", 0, 1):
             up = grp[(1, key)][:].rearrange("p (a c e) -> p a c e", c=64, e=4)
-            nc.vector.memset(up[:, :, 62:64, :], 0.0)
+            nc.vector.memset(up[:, :, 60:64, :], 0.0)
             dn = grp[(-1, key)][:].rearrange("p (a c e) -> p a c e", c=64, e=4)
-            nc.vector.memset(dn[:, :, 0:2, :], 0.0)
+            nc.vector.memset(dn[:, :, 0:4, :], 0.0)
+        nc.vector.tensor_reduce(out=mask_even[:], in_=id_pairs[:, :, 0], axis=mybir.AxisListType.X, op=ADD)
+        nc.vector.tensor_reduce(out=mask_odd[:], in_=id_pairs[:, :, 1], axis=mybir.AxisListType.X, op=ADD)
 
         codes = {}
         scales = {}
         for s in SHIFTS:
-            codes[s] = keep.tile([P, (NT + 1) * P], U32, name="codes%d" % (s + 1), align_bytes=64)
-            scales[s] = keep.tile([P, (NT + 1) * P], U8, name="scales%d" % (s + 1), align_bytes=64)
+            codes[s] = keep.tile([P, (XS + 1) * P], U32, name="codes%d" % (s + 1), align_bytes=64)
+            scales[s] = keep.tile([P, (XS + 1) * P], U8, name="scales%d" % (s + 1), align_bytes=64)
         w_grp = keep.tile([P, FEAT * 4], BF16, name="w_grp", align_bytes=64)
         w_codes = keep.tile([P, FEAT], U32, name="w_codes", align_bytes=64)
         w_scales = keep.tile([P, FEAT], U8, name="w_scales", align_bytes=64)
-        cx = keep.tile([P, FEAT], F32, name="cx")
+        cx = keep.tile([P, 2, HALF], F32, name="cx")
+        b_first = keep.tile([P, 2, HALF], F32, name="b_first")
+        ring = keep.tile([P, RING, 6, HALF], F32, name="ring")
 
-        def transpose_pair(xt, src32, first, count):
+        def transposes(tag, src32, first, count):
+            xt = psum.tile([P, 2, 256], F32, tag=tag, bufs=(2 if tag == "xt" else 3), name="xt")
             for jj in range(count):
                 for u in range(2):
                     lo = (first + jj) * 256 + u * P
                     nc.tensor.transpose(xt[:, u, jj * P:(jj + 1) * P], src32[:, lo:lo + P], ident[:])
+            return xt
 
-        def prep_w(h):
-            w32 = w_sb[:].bitcast(F32)
-            wg32 = w_grp[:].bitcast(F32)
-            for jp in (2 * h, 2 * h + 1):
-                xt = psum.tile([P, 2, 256], F32, tag="xt", bufs=2, name="xt")
-                transpose_pair(xt, w32, 2 * jp, 2)
-                nc.vector.tensor_copy(
-                    out=wg32[:, jp * 512:(jp + 1) * 512].rearrange("p (f u) -> p f u", u=2),
-                    in_=xt[:].rearrange("p u f -> p f u"),
-                )
+        def w_out(xt, jp):
+            nc.vector.tensor_copy(
+                out=w_grp[:].bitcast(F32)[:, jp * 512:(jp + 1) * 512].rearrange("p (f u) -> p f u", u=2),
+                in_=xt[:].rearrange("p u f -> p f u"),
+            )
+
+        def w_quantise(h):
             nc.vector.quantize_mx(
                 out=w_codes[:, h * 512:(h + 1) * 512].bitcast(E4X4),
                 scales=w_scales[:, h * 512:(h + 1) * 512],
                 in_=w_grp[:, h * 2048:(h + 1) * 2048],
             )
 
-        def regroup(xt, ntile, key, word0):
+        def regroup(xt, ntile, key, word0, s):
             src = xt[:, :, 0:ntile * P].rearrange("p u (a c) -> p a c u", c=64)
-            for s in SHIFTS:
-                dst = grp[(s, key)][:].bitcast(F32)[:, word0:word0 + ntile * 256].rearrange(
-                    "p (a c u) -> p a c u", c=64, u=2)
-                if s == 0:
-                    nc.scalar.copy(out=dst, in_=src)
-                elif s == 1:
-                    nc.scalar.copy(out=dst[:, :, 0:62, :], in_=src[:, :, 2:64, :])
-                else:
-                    nc.scalar.copy(out=dst[:, :, 2:64, :], in_=src[:, :, 0:62, :])
+            dst = grp[(s, key)][:].bitcast(F32)[:, word0:word0 + ntile * 256].rearrange(
+                "p (a c u) -> p a c u", c=64, u=2)
+            if s == 0:
+                nc.scalar.copy(out=dst, in_=src)
+            elif s == 1:
+                nc.scalar.copy(out=dst[:, :, 0:62, :], in_=src[:, :, 2:64, :])
+            else:
+                nc.scalar.copy(out=dst[:, :, 2:64, :], in_=src[:, :, 0:62, :])
 
-        def quantise(key, slot0, ntile):
+        def quantise(key, col0, slot0, ntile):
             for s in SHIFTS:
                 nc.vector.quantize_mx(
                     out=codes[s][:, slot0 * P:(slot0 + ntile) * P].bitcast(E5X4),
                     scales=scales[s][:, slot0 * P:(slot0 + ntile) * P],
-                    in_=grp[(s, key)][:, 0:ntile * P * 4],
+                    in_=grp[(s, key)][:, col0:col0 + ntile * P * 4],
                 )
-
-        def prep_x():
-            xt = psum.tile([P, 2, 256], F32, tag="xt", bufs=2, name="xt")
-            transpose_pair(xt, gx_sb[:].bitcast(F32), 0, 1)
-            regroup(xt, 1, "x", 0)
-            quantise("x", XS, 1)
-
-        def prep_g(g):
-            g32 = g_sb[g][:].bitcast(F32)
-            for bk in range(GROUPS[g][1] // 2):
-                xt = psum.tile([P, 2, 256], F32, tag="xt", bufs=2, name="xt")
-                transpose_pair(xt, g32, 2 * bk, 2)
-                regroup(xt, 2, g % 2, bk * 512)
-            quantise(g % 2, GROUPS[g][0], GROUPS[g][1])
 
         def mx(acc, s, slot, fh, start, stop):
             nc.tensor.matmul_mx(
@@ -171,68 +158,99 @@ def tile_graphconvlayer_t_kernel(tc, X, Wm, b, H, W, grad_out, out):
             )
 
         def column_sum_direct(slot, fh, dst):
-            pb = psum.tile([P, 512], F32, tag="pb", bufs=3, name="pb")
+            pb = psum.tile([P, HALF], F32, tag="pb", bufs=3, name="pb")
             mx(pb, -1, slot, fh, True, False)
             mx(pb, 0, slot, fh, False, False)
             mx(pb, 1, slot, fh, False, True)
             nc.scalar.copy(out=dst, in_=pb[:])
 
-        prep_w(0)
-        prep_g(0)
-        prep_x()
-        prep_w(1)
+        w32 = w_sb[:].bitcast(F32)
+        xw = [transposes("xt", w32, 0, 2), transposes("xt", w32, 2, 2)]
+        xx = transposes("pa", gx_sb[:].bitcast(F32), 0, 1)
+        g32 = g_sb[0][:].bitcast(F32)
+        xg = [transposes("pa", g32, 0, 2), transposes("pa", g32, 2, 2)]
+        w_out(xw[0], 0)
+        w_out(xw[1], 1)
+        w_quantise(0)
+        for s in SHIFTS:
+            regroup(xx, 1, "x", 0, s)
+        for s in SHIFTS:
+            regroup(xg[0], 2, 0, 0, s)
+        quantise("x", 0, XS, 1)
+        xw = [transposes("pb", w32, 4, 2), transposes("pb", w32, 6, 2)]
+        quantise(0, 0, 0, 2)
+        w_out(xw[0], 2)
+        w_out(xw[1], 3)
+        w_quantise(1)
+        for s in SHIFTS:
+            regroup(xg[1], 2, 0, 512, s)
+        quantise(0, 1024, 2, 2)
         for fh in range(2):
-            column_sum_direct(XS, fh, cx[:, fh * 512:(fh + 1) * 512])
-
-        csum = {}
-        stage = {}
+            column_sum_direct(XS, fh, cx[:, fh, :])
 
         def unit(t, fh):
-            fs = slice(fh * 512, (fh + 1) * 512)
-            pa = psum.tile([P, 512], F32, tag="pa", bufs=3, name="pa")
-            mx(pa, -1, t, fh, True, False)
-            mx(pa, 1, t, fh, False, True)
-            d_dst = stage[t // 2][:, t % 2, fs]
+            e = t % RING
+            ep = (t - 1) % RING
             if is_direct(t, fh):
-                column_sum_direct(t, fh, csum[t][:, fs])
-                bsb = None
+                column_sum_direct(t % XS, fh, ring[:, e, 2 + fh, :])
             else:
-                pb = psum.tile([P, 512], F32, tag="pb", bufs=3, name="pb")
-                mx(pb, 0, t, fh, True, True)
-                bsb = work.tile([P, 512], F32, tag="bsb", bufs=4, name="bsb")
-                nc.scalar.copy(out=bsb[:], in_=pb[:])
+                pb = psum.tile([P, HALF], F32, tag="pb", bufs=3, name="pb")
+                mx(pb, 0, t % XS, fh, True, True)
+                nc.scalar.copy(out=(b_first[:, fh, :] if t == 0 else ring[:, ep, 4 + fh, :]), in_=pb[:])
+            pa = psum.tile([P, HALF], F32, tag="pa", bufs=3, name="pa")
+            mx(pa, -1, t % XS, fh, True, False)
+            mx(pa, 1, t % XS, fh, False, True)
             if t == 0:
                 nc.vector.scalar_tensor_tensor(
-                    out=d_dst, in0=cx[:, fs], scalar=mask_odd[:, 0:1], in1=pa[:], op0=MULT, op1=ADD)
+                    out=ring[:, e, fh, :], in0=cx[:, fh, :], scalar=mask_odd[:, 0:1], in1=pa[:], op0=MULT, op1=ADD)
+                nc.vector.tensor_tensor(out=ring[:, e, 2 + fh, :], in0=pa[:], in1=b_first[:, fh, :], op=ADD)
+            elif is_direct(t, fh):
+                nc.vector.tensor_tensor(out=ring[:, e, fh, :], in0=pa[:], in1=ring[:, ep, 2 + fh, :], op=ADD)
             else:
-                nc.vector.tensor_tensor(out=d_dst, in0=pa[:], in1=csum[t - 1][:, fs], op=ADD)
-            if bsb is not None:
-                nc.vector.tensor_tensor(out=csum[t][:, fs], in0=pa[:], in1=bsb[:], op=ADD)
+                nc.vector.tensor_tensor(
+                    out=ring[:, e, fh:fh + 3:2, :],
+                    in0=pa[:].unsqueeze(1).to_broadcast([P, 2, HALF]),
+                    in1=ring[:, ep, 2 + fh:2 + fh + 3:2, :],
+                    op=ADD,
+                )
 
         def finish(t):
-            dst = stage[t // 2][:, t % 2, :]
+            e = t % RING
+            dst = ring[:, e, 0:2, :]
             if t == NT - 1:
                 nc.vector.scalar_tensor_tensor(
                     out=dst, in0=cx[:], scalar=mask_even[:, 0:1], in1=dst, op0=MULT, op1=ADD)
             elif on_vector(t):
-                nc.vector.tensor_tensor(out=dst, in0=dst, in1=csum[t + 1][:], op=ADD)
+                nc.vector.tensor_tensor(out=dst, in0=dst, in1=ring[:, (t + 1) % RING, 2:4, :], op=ADD)
             else:
-                nc.gpsimd.tensor_tensor(out=dst, in0=dst, in1=csum[t + 1][:], op=ADD)
-            if t >= NT - 2:
-                nc.sync.dma_start(out=out_pt[:, t, :], in_=dst)
-            elif t % 2 == 1:
-                nc.sync.dma_start(out=out_pt[:, t - 1:t + 1, :], in_=stage[t // 2][:])
+                nc.gpsimd.tensor_tensor(out=dst, in0=dst, in1=ring[:, (t + 1) % RING, 2:4, :], op=ADD)
 
-        for g in range(len(GROUPS)):
-            if g + 1 < len(GROUPS):
-                prep_g(g + 1)
-            for t in range(GROUPS[g][0], GROUPS[g][0] + GROUPS[g][1]):
-                csum[t] = work.tile([P, FEAT], F32, tag="csum", bufs=5, name="csum")
-                if t % 2 == 0:
-                    stage[t // 2] = work.tile([P, 2, FEAT], F32, tag="stage", bufs=4, name="stage")
-                for fh in range(2):
-                    unit(t, fh)
-                if t == NT - 1:
-                    finish(t)
-                if t >= 1:
+        def store(t, n):
+            e = t % RING
+            nc.sync.dma_start(
+                out=out_pt[:, t:t + n, :],
+                in_=ring[:, e:e + n, 0:2, :].rearrange("p a s f -> p a (s f)"),
+            )
+
+        for g in range(NG):
+            more = g + 1 < NG
+            if more:
+                g32 = g_sb[g + 1][:].bitcast(F32)
+                xg = [transposes("xt", g32, 0, 2), transposes("xt", g32, 2, 2)]
+            for n in range(2 * GRP):
+                t = g * GRP + n // 2
+                unit(t, n % 2)
+                if more and n < 6:
+                    regroup(xg[n // 3], 2, (g + 1) % 2, (n // 3) * 512, SHIFTS[n % 3])
+                if n % 2 == 1 and t >= 1 and not on_vector(t - 1):
                     finish(t - 1)
+                if n == 5:
+                    if more:
+                        quantise((g + 1) % 2, 0, ((g + 1) % 2) * GRP, GRP)
+                    finish(t - 1)
+                if n % 2 == 1 and t >= 2 and t % 2 == 0:
+                    store(t - 2, 2)
+        finish(NT - 1)
+        store(NT - 1, 1)
+        finish(NT - 2)
+        store(NT - 2, 1)

@@ -26,10 +26,11 @@ FLOPS = 2 * NODES * K * FEAT
 BYTES = NODES * K * 2 + FEAT * K * 2 + NODES * FEAT * 4
 
 SHIFTS = (-1, 0, 1)
+BANKS = {"xt": 2, "pa": 4, "pb": 2}
 
 
 def is_direct(t, fh):
-    return fh == 1 and t % 4 != 0
+    return fh == 1 and t > 0
 
 
 def on_vector(t):
@@ -107,7 +108,7 @@ def tile_graphconvlayer_t_kernel(tc, X, Wm, b, H, W, grad_out, out):
         ring = keep.tile([P, RING, 6, HALF], F32, name="ring")
 
         def transposes(tag, src32, first, count):
-            xt = psum.tile([P, 2, 256], F32, tag=tag, bufs=(2 if tag == "xt" else 3), name="xt")
+            xt = psum.tile([P, 2, 256], F32, tag=tag, bufs=BANKS[tag], name="xt")
             for jj in range(count):
                 for u in range(2):
                     lo = (first + jj) * 256 + u * P
@@ -158,7 +159,7 @@ def tile_graphconvlayer_t_kernel(tc, X, Wm, b, H, W, grad_out, out):
             )
 
         def column_sum_direct(slot, fh, dst):
-            pb = psum.tile([P, HALF], F32, tag="pb", bufs=3, name="pb")
+            pb = psum.tile([P, HALF], F32, tag="pb", bufs=BANKS["pb"], name="pb")
             mx(pb, -1, slot, fh, True, False)
             mx(pb, 0, slot, fh, False, False)
             mx(pb, 1, slot, fh, False, True)
@@ -194,10 +195,10 @@ def tile_graphconvlayer_t_kernel(tc, X, Wm, b, H, W, grad_out, out):
             if is_direct(t, fh):
                 column_sum_direct(t % XS, fh, ring[:, e, 2 + fh, :])
             else:
-                pb = psum.tile([P, HALF], F32, tag="pb", bufs=3, name="pb")
+                pb = psum.tile([P, HALF], F32, tag="pb", bufs=BANKS["pb"], name="pb")
                 mx(pb, 0, t % XS, fh, True, True)
                 nc.scalar.copy(out=(b_first[:, fh, :] if t == 0 else ring[:, ep, 4 + fh, :]), in_=pb[:])
-            pa = psum.tile([P, HALF], F32, tag="pa", bufs=3, name="pa")
+            pa = psum.tile([P, HALF], F32, tag="pa", bufs=BANKS["pa"], name="pa")
             mx(pa, -1, t % XS, fh, True, False)
             mx(pa, 1, t % XS, fh, False, True)
             if t == 0:

@@ -7,10 +7,11 @@ F32 = mybir.dt.float32
 BF16 = mybir.dt.bfloat16
 U32 = mybir.dt.uint32
 U8 = mybir.dt.uint8
+I32 = mybir.dt.int32
 E5X4 = mybir.dt.float8_e5m2_x4
 E4X4 = mybir.dt.float8_e4m3fn_x4
 ADD = mybir.AluOpType.add
-MULT = mybir.AluOpType.mult
+COPY = mybir.ActivationFunctionType.Copy
 
 P = 128
 NODES = 4096
@@ -18,10 +19,11 @@ K = 512
 FEAT = 1024
 HALF = 512
 NT = 32
-XS = 8
 GRP = 4
 NG = NT // GRP
+AHEAD = 2
 RING = 8
+STEP = 4
 FLOPS = 2 * NODES * K * FEAT
 BYTES = NODES * K * 2 + FEAT * K * 2 + NODES * FEAT * 4
 
@@ -30,11 +32,17 @@ BANKS = {"xt": 2, "pa": 4, "pb": 2}
 
 
 def is_direct(t, fh):
-    return fh == 1 and t > 0
+    return t >= NT - 4 or (fh == 1 and t % 3 != 0)
 
 
-def on_vector(t):
-    return t % 4 == 1 or t >= NT - 2
+def last_add(t, fh):
+    if t == NT - 1:
+        return "v"
+    if t >= NT - 5:
+        return "p" if is_direct(t + 1, fh) else "v"
+    if fh == 1 and t % 6 == 1:
+        return "p"
+    return "g"
 
 
 def tile_graphconvlayer_t_kernel(tc, X, Wm, b, H, W, grad_out, out):
@@ -44,7 +52,7 @@ def tile_graphconvlayer_t_kernel(tc, X, Wm, b, H, W, grad_out, out):
     g_pt = g_flat.rearrange("(p t) k -> p t k", t=NT)
     g_mc = g_flat.rearrange("(m c) k -> m c k", c=64)
     w_pj = Wm.rearrange("(j p) k -> p j k", p=P)
-    out_pt = out.flatten_outer_dims().rearrange("(p t) f -> p t f", t=NT)
+    out_q = out.rearrange("i (r h t) f -> i h r t f", h=2, t=NT)
 
     with ExitStack() as ctx:
         keep = ctx.enter_context(tc.tile_pool(name="keep", bufs=1))
@@ -66,59 +74,58 @@ def tile_graphconvlayer_t_kernel(tc, X, Wm, b, H, W, grad_out, out):
                 in_=g_pt[:, g * GRP:(g + 1) * GRP, :],
             )
 
-        load_w(0)
+        load_g(0)
         nc.sync.dma_start(out=gx_sb[0:P:2, :], in_=g_mc[:, 32, :])
         nc.sync.dma_start(out=gx_sb[1:P:2, :], in_=g_mc[:, 31, :])
-        load_g(0)
+        load_w(0)
         load_w(1)
         for g in range(1, NG):
             load_g(g)
 
         ctx.enter_context(tc.manual_schedule())
 
-        ident = keep.tile([P, P], F32, name="ident")
-        make_identity(nc, ident[:])
-        id_pairs = ident[:].rearrange("p (a e) -> p a e", e=2)
-        mask_even = keep.tile([P, 1], F32, name="mask_even")
-        mask_odd = keep.tile([P, 1], F32, name="mask_odd")
-
-        grp = {}
-        for s in SHIFTS:
-            for bb in range(2):
-                grp[(s, bb)] = keep.tile([P, GRP * P * 4], BF16, name="grp%d_%d" % (s + 1, bb), align_bytes=64)
-            grp[(s, "x")] = keep.tile([P, P * 4], BF16, name="grpx%d" % (s + 1), align_bytes=64)
-        for key in ("x", 0, 1):
-            up = grp[(1, key)][:].rearrange("p (a c e) -> p a c e", c=64, e=4)
-            nc.vector.memset(up[:, :, 60:64, :], 0.0)
-            dn = grp[(-1, key)][:].rearrange("p (a c e) -> p a c e", c=64, e=4)
-            nc.vector.memset(dn[:, :, 0:4, :], 0.0)
-        nc.vector.tensor_reduce(out=mask_even[:], in_=id_pairs[:, :, 0], axis=mybir.AxisListType.X, op=ADD)
-        nc.vector.tensor_reduce(out=mask_odd[:], in_=id_pairs[:, :, 1], axis=mybir.AxisListType.X, op=ADD)
-
         codes = {}
         scales = {}
         for s in SHIFTS:
-            codes[s] = keep.tile([P, (XS + 1) * P], U32, name="codes%d" % (s + 1), align_bytes=64)
-            scales[s] = keep.tile([P, (XS + 1) * P], U8, name="scales%d" % (s + 1), align_bytes=64)
+            codes[s] = keep.tile([P, (NT + 1) * P], U32, name="codes%d" % (s + 1), align_bytes=64)
+            scales[s] = keep.tile([P, (NT + 1) * P], U8, name="scales%d" % (s + 1), align_bytes=64)
+            nc.vector.memset(scales[s][:].bitcast(I32), 0)
+        nc.vector.memset(codes[1][:].bitcast(I32).rearrange("p (a c) -> p a c", c=P)[:, :, P - STEP:P], 0)
+        nc.vector.memset(codes[-1][:].bitcast(I32).rearrange("p (a c) -> p a c", c=P)[:, :, 0:STEP], 0)
+
+        ident = keep.tile([P, P], F32, name="ident")
+        make_identity(nc, ident[:])
+        perm = keep.tile([P, P], F32, name="perm")
+        nc.vector.tensor_copy(
+            out=perm[:].rearrange("p (r i h) -> p r i h", i=2, h=2),
+            in_=ident[:].rearrange("p (i r h) -> p r i h", i=2, h=2),
+        )
+        id_pairs = ident[:].rearrange("p (a e) -> p a e", e=2)
+        mask_even = keep.tile([P, 1], F32, name="mask_even")
+        mask_odd = keep.tile([P, 1], F32, name="mask_odd")
+        nc.vector.tensor_reduce(out=mask_even[:], in_=id_pairs[:, :, 0], axis=mybir.AxisListType.X, op=ADD)
+        nc.vector.tensor_reduce(out=mask_odd[:], in_=id_pairs[:, :, 1], axis=mybir.AxisListType.X, op=ADD)
+
+        grp = [keep.tile([P, GRP * P * 4], BF16, name="grp%d" % bb, align_bytes=64) for bb in range(2)]
+        grpx = keep.tile([P, P * 4], BF16, name="grpx", align_bytes=64)
         w_grp = keep.tile([P, FEAT * 4], BF16, name="w_grp", align_bytes=64)
         w_codes = keep.tile([P, FEAT], U32, name="w_codes", align_bytes=64)
         w_scales = keep.tile([P, FEAT], U8, name="w_scales", align_bytes=64)
-        cx = keep.tile([P, 2, HALF], F32, name="cx")
-        b_first = keep.tile([P, 2, HALF], F32, name="b_first")
+        c_end = keep.tile([P, 2, HALF], F32, name="c_end")
         ring = keep.tile([P, RING, 6, HALF], F32, name="ring")
 
-        def transposes(tag, src32, first, count):
+        def transposes(tag, src32, first, count, mat):
             xt = psum.tile([P, 2, 256], F32, tag=tag, bufs=BANKS[tag], name="xt")
             for jj in range(count):
                 for u in range(2):
                     lo = (first + jj) * 256 + u * P
-                    nc.tensor.transpose(xt[:, u, jj * P:(jj + 1) * P], src32[:, lo:lo + P], ident[:])
+                    nc.tensor.transpose(xt[:, u, jj * P:(jj + 1) * P], src32[:, lo:lo + P], mat[:])
             return xt
 
-        def w_out(xt, jp):
-            nc.vector.tensor_copy(
-                out=w_grp[:].bitcast(F32)[:, jp * 512:(jp + 1) * 512].rearrange("p (f u) -> p f u", u=2),
-                in_=xt[:].rearrange("p u f -> p f u"),
+        def regroup(engine, xt, ntile, dst, word0):
+            engine(
+                out=dst[:].bitcast(F32)[:, word0:word0 + ntile * 256].rearrange("p (n u) -> p n u", u=2),
+                in_=xt[:, :, 0:ntile * P].rearrange("p u n -> p n u"),
             )
 
         def w_quantise(h):
@@ -128,24 +135,33 @@ def tile_graphconvlayer_t_kernel(tc, X, Wm, b, H, W, grad_out, out):
                 in_=w_grp[:, h * 2048:(h + 1) * 2048],
             )
 
-        def regroup(xt, ntile, key, word0, s):
-            src = xt[:, :, 0:ntile * P].rearrange("p u (a c) -> p a c u", c=64)
-            dst = grp[(s, key)][:].bitcast(F32)[:, word0:word0 + ntile * 256].rearrange(
-                "p (a c u) -> p a c u", c=64, u=2)
-            if s == 0:
-                nc.scalar.copy(out=dst, in_=src)
-            elif s == 1:
-                nc.scalar.copy(out=dst[:, :, 0:62, :], in_=src[:, :, 2:64, :])
-            else:
-                nc.scalar.copy(out=dst[:, :, 2:64, :], in_=src[:, :, 0:62, :])
+        def quantise(src, slot0, ntile):
+            nc.vector.quantize_mx(
+                out=codes[0][:, slot0 * P:(slot0 + ntile) * P].bitcast(E5X4),
+                scales=scales[0][:, slot0 * P:(slot0 + ntile) * P],
+                in_=src[:, 0:ntile * P * 4],
+            )
 
-        def quantise(key, col0, slot0, ntile):
-            for s in SHIFTS:
-                nc.vector.quantize_mx(
-                    out=codes[s][:, slot0 * P:(slot0 + ntile) * P].bitcast(E5X4),
-                    scales=scales[s][:, slot0 * P:(slot0 + ntile) * P],
-                    in_=grp[(s, key)][:, col0:col0 + ntile * P * 4],
-                )
+        def move(slot0, ntile, by_dma):
+            lo = slot0 * P
+            hi = (slot0 + ntile) * P
+            mid = codes[0][:].bitcast(I32)[:, lo:hi].rearrange("p (a c) -> p a c", c=P)
+            up = codes[1][:].bitcast(I32)[:, lo:hi].rearrange("p (a c) -> p a c", c=P)
+            dn = codes[-1][:].bitcast(I32)[:, lo:hi].rearrange("p (a c) -> p a c", c=P)
+            wlo = lo // 4
+            whi = hi // 4
+            smid = scales[0][:].bitcast(I32)
+            pairs = [
+                (up[:, :, 0:P - STEP], mid[:, :, STEP:P]),
+                (dn[:, :, STEP:P], mid[:, :, 0:P - STEP]),
+                (scales[1][:].bitcast(I32)[:, wlo:whi - 1], smid[:, wlo + 1:whi]),
+                (scales[-1][:].bitcast(I32)[:, wlo + 1:whi], smid[:, wlo:whi - 1]),
+            ]
+            for dst, src in pairs:
+                if by_dma:
+                    nc.sync.dma_start(out=dst, in_=src)
+                else:
+                    nc.vector.tensor_copy(out=dst, in_=src)
 
         def mx(acc, s, slot, fh, start, stop):
             nc.tensor.matmul_mx(
@@ -158,54 +174,53 @@ def tile_graphconvlayer_t_kernel(tc, X, Wm, b, H, W, grad_out, out):
                 stop=stop,
             )
 
-        def column_sum_direct(slot, fh, dst):
+        def column_sum(slot, fh):
             pb = psum.tile([P, HALF], F32, tag="pb", bufs=BANKS["pb"], name="pb")
             mx(pb, -1, slot, fh, True, False)
             mx(pb, 0, slot, fh, False, False)
             mx(pb, 1, slot, fh, False, True)
-            nc.scalar.copy(out=dst, in_=pb[:])
+            return pb
 
         w32 = w_sb[:].bitcast(F32)
-        xw = [transposes("xt", w32, 0, 2), transposes("xt", w32, 2, 2)]
-        xx = transposes("pa", gx_sb[:].bitcast(F32), 0, 1)
         g32 = g_sb[0][:].bitcast(F32)
-        xg = [transposes("pa", g32, 0, 2), transposes("pa", g32, 2, 2)]
-        w_out(xw[0], 0)
-        w_out(xw[1], 1)
+        xg = [transposes("pa", g32, 0, 2, perm), transposes("pa", g32, 2, 2, perm)]
+        xx = transposes("pa", gx_sb[:].bitcast(F32), 0, 1, perm)
+        regroup(nc.scalar.copy, xg[0], 2, grp[0], 0)
+        regroup(nc.vector.tensor_copy, xg[1], 2, grp[0], 512)
+        regroup(nc.scalar.copy, xx, 1, grpx, 0)
+        quantise(grp[0], 1, GRP)
+        quantise(grpx, 0, 1)
+        xw = [transposes("xt", w32, 0, 2, ident), transposes("xt", w32, 2, 2, ident)]
+        move(0, GRP + 1, False)
+        regroup(nc.scalar.copy, xw[0], 2, w_grp, 0)
+        regroup(nc.scalar.copy, xw[1], 2, w_grp, 512)
         w_quantise(0)
-        for s in SHIFTS:
-            regroup(xx, 1, "x", 0, s)
-        for s in SHIFTS:
-            regroup(xg[0], 2, 0, 0, s)
-        quantise("x", 0, XS, 1)
-        xw = [transposes("pb", w32, 4, 2), transposes("pb", w32, 6, 2)]
-        quantise(0, 0, 0, 2)
-        w_out(xw[0], 2)
-        w_out(xw[1], 3)
+        xw = [transposes("pb", w32, 4, 2, ident), transposes("pb", w32, 6, 2, ident)]
+        regroup(nc.scalar.copy, xw[0], 2, w_grp, 1024)
+        regroup(nc.scalar.copy, xw[1], 2, w_grp, 1536)
         w_quantise(1)
-        for s in SHIFTS:
-            regroup(xg[1], 2, 0, 512, s)
-        quantise(0, 1024, 2, 2)
         for fh in range(2):
-            column_sum_direct(XS, fh, cx[:, fh, :])
+            pb = column_sum(0, fh)
+            nc.scalar.activation(out=ring[:, RING - 1, 2 + fh, :], in_=pb[:], func=COPY, scale=mask_odd[:, 0:1])
+            nc.scalar.activation(out=c_end[:, fh, :], in_=pb[:], func=COPY, scale=mask_even[:, 0:1])
 
         def unit(t, fh):
             e = t % RING
             ep = (t - 1) % RING
             if is_direct(t, fh):
-                column_sum_direct(t % XS, fh, ring[:, e, 2 + fh, :])
+                pb = column_sum(t + 1, fh)
+                if t < NT - 1:
+                    nc.scalar.copy(out=ring[:, e, 2 + fh, :], in_=pb[:])
+                if t >= 1 and last_add(t - 1, fh) == "p":
+                    nc.vector.tensor_tensor(out=ring[:, ep, fh, :], in0=pb[:], in1=ring[:, ep, fh, :], op=ADD)
             else:
                 pb = psum.tile([P, HALF], F32, tag="pb", bufs=BANKS["pb"], name="pb")
-                mx(pb, 0, t % XS, fh, True, True)
-                nc.scalar.copy(out=(b_first[:, fh, :] if t == 0 else ring[:, ep, 4 + fh, :]), in_=pb[:])
+                mx(pb, 0, t + 1, fh, True, True)
+                nc.scalar.copy(out=ring[:, ep, 4 + fh, :], in_=pb[:])
             pa = psum.tile([P, HALF], F32, tag="pa", bufs=BANKS["pa"], name="pa")
-            mx(pa, -1, t % XS, fh, True, False)
-            mx(pa, 1, t % XS, fh, False, True)
-            if t == 0:
-                nc.vector.scalar_tensor_tensor(
-                    out=ring[:, e, fh, :], in0=cx[:, fh, :], scalar=mask_odd[:, 0:1], in1=pa[:], op0=MULT, op1=ADD)
-                nc.vector.tensor_tensor(out=ring[:, e, 2 + fh, :], in0=pa[:], in1=b_first[:, fh, :], op=ADD)
-            elif is_direct(t, fh):
+            mx(pa, -1, t + 1, fh, True, False)
+            mx(pa, 1, t + 1, fh, False, True)
+            if is_direct(t, fh):
                 nc.vector.tensor_tensor(out=ring[:, e, fh, :], in0=pa[:], in1=ring[:, ep, 2 + fh, :], op=ADD)
             else:
                 nc.vector.tensor_tensor(
@@ -216,42 +231,47 @@ def tile_graphconvlayer_t_kernel(tc, X, Wm, b, H, W, grad_out, out):
                 )
 
         def finish(t):
-            e = t % RING
-            dst = ring[:, e, 0:2, :]
-            if t == NT - 1:
-                nc.vector.scalar_tensor_tensor(
-                    out=dst, in0=cx[:], scalar=mask_even[:, 0:1], in1=dst, op0=MULT, op1=ADD)
-            elif on_vector(t):
-                nc.vector.tensor_tensor(out=dst, in0=dst, in1=ring[:, (t + 1) % RING, 2:4, :], op=ADD)
-            else:
-                nc.gpsimd.tensor_tensor(out=dst, in0=dst, in1=ring[:, (t + 1) % RING, 2:4, :], op=ADD)
+            for how, engine in (("g", nc.gpsimd), ("v", nc.vector)):
+                halves = [fh for fh in range(2) if last_add(t, fh) == how]
+                if halves:
+                    lo = halves[0]
+                    hi = halves[-1] + 1
+                    dst = ring[:, t % RING, lo:hi, :]
+                    nxt = c_end[:, lo:hi, :] if t == NT - 1 else ring[:, (t + 1) % RING, 2 + lo:2 + hi, :]
+                    engine.tensor_tensor(out=dst, in0=dst, in1=nxt, op=ADD)
 
         def store(t, n):
             e = t % RING
-            nc.sync.dma_start(
-                out=out_pt[:, t:t + n, :],
-                in_=ring[:, e:e + n, 0:2, :].rearrange("p a s f -> p a (s f)"),
-            )
+            for q in range(4):
+                nc.sync.dma_start(
+                    out=out_q[q // 2, q % 2, :, t:t + n, :],
+                    in_=ring[q:P:4, e:e + n, 0:2, :].rearrange("p a s f -> p a (s f)"),
+                )
 
-        for g in range(NG):
-            more = g + 1 < NG
-            if more:
-                g32 = g_sb[g + 1][:].bitcast(F32)
-                xg = [transposes("xt", g32, 0, 2), transposes("xt", g32, 2, 2)]
-            for n in range(2 * GRP):
-                t = g * GRP + n // 2
-                unit(t, n % 2)
-                if more and n < 6:
-                    regroup(xg[n // 3], 2, (g + 1) % 2, (n // 3) * 512, SHIFTS[n % 3])
-                if n % 2 == 1 and t >= 1 and not on_vector(t - 1):
-                    finish(t - 1)
-                if n == 5:
-                    if more:
-                        quantise((g + 1) % 2, 0, ((g + 1) % 2) * GRP, GRP)
-                    finish(t - 1)
-                if n % 2 == 1 and t >= 2 and t % 2 == 0:
-                    store(t - 2, 2)
+        first_unit = {1: 0, 2: GRP}
+        starts = {0: 1, GRP: 2}
+        for k in range(3, NG):
+            first_unit[k] = (k - AHEAD) * 2 * GRP
+            starts[(k - AHEAD) * 2 * GRP] = k
+        k = 0
+        for u in range(2 * NT):
+            t = u // 2
+            if u in starts:
+                k = starts[u]
+                g32 = g_sb[k][:].bitcast(F32)
+                xg = [transposes("xt", g32, 0, 2, perm), transposes("xt", g32, 2, 2, perm)]
+            unit(t, u % 2)
+            step = u - first_unit[k] if k else 9
+            if step < 2:
+                regroup(nc.scalar.copy, xg[step], 2, grp[k % 2], step * 512)
+            if step == 2:
+                quantise(grp[k % 2], 1 + k * GRP, GRP)
+                move(1 + k * GRP, GRP, True)
+            if u % 2 == 1 and t >= 1:
+                finish(t - 1)
+            if u % 2 == 1 and 2 <= t <= NT - GRP and t % 2 == 0:
+                store(t - 2, 2)
+            if u % 2 == 1 and t > NT - GRP:
+                store(t - 1, 1)
         finish(NT - 1)
         store(NT - 1, 1)
-        finish(NT - 2)
-        store(NT - 2, 1)

@@ -11,7 +11,7 @@ I32 = mybir.dt.int32
 E5X4 = mybir.dt.float8_e5m2_x4
 E4X4 = mybir.dt.float8_e4m3fn_x4
 ADD = mybir.AluOpType.add
-COPY = mybir.ActivationFunctionType.Copy
+MULT = mybir.AluOpType.mult
 
 P = 128
 NODES = 4096
@@ -84,6 +84,13 @@ def tile_graphconvlayer_t_kernel(tc, X, Wm, b, H, W, grad_out, out):
 
         ctx.enter_context(tc.manual_schedule())
 
+        ident = keep.tile([P, P], F32, name="ident")
+        make_identity(nc, ident[:])
+        perm = keep.tile([P, P], F32, name="perm")
+        nc.vector.tensor_copy(
+            out=perm[:].rearrange("p (r i h) -> p r i h", i=2, h=2),
+            in_=ident[:].rearrange("p (i r h) -> p r i h", i=2, h=2),
+        )
         codes = {}
         scales = {}
         for s in SHIFTS:
@@ -92,14 +99,6 @@ def tile_graphconvlayer_t_kernel(tc, X, Wm, b, H, W, grad_out, out):
             nc.vector.memset(scales[s][:].bitcast(I32), 0)
         nc.vector.memset(codes[1][:].bitcast(I32).rearrange("p (a c) -> p a c", c=P)[:, :, P - STEP:P], 0)
         nc.vector.memset(codes[-1][:].bitcast(I32).rearrange("p (a c) -> p a c", c=P)[:, :, 0:STEP], 0)
-
-        ident = keep.tile([P, P], F32, name="ident")
-        make_identity(nc, ident[:])
-        perm = keep.tile([P, P], F32, name="perm")
-        nc.vector.tensor_copy(
-            out=perm[:].rearrange("p (r i h) -> p r i h", i=2, h=2),
-            in_=ident[:].rearrange("p (i r h) -> p r i h", i=2, h=2),
-        )
         id_pairs = ident[:].rearrange("p (a e) -> p a e", e=2)
         mask_even = keep.tile([P, 1], F32, name="mask_even")
         mask_odd = keep.tile([P, 1], F32, name="mask_odd")
@@ -111,7 +110,7 @@ def tile_graphconvlayer_t_kernel(tc, X, Wm, b, H, W, grad_out, out):
         w_grp = keep.tile([P, FEAT * 4], BF16, name="w_grp", align_bytes=64)
         w_codes = keep.tile([P, FEAT], U32, name="w_codes", align_bytes=64)
         w_scales = keep.tile([P, FEAT], U8, name="w_scales", align_bytes=64)
-        c_end = keep.tile([P, 2, HALF], F32, name="c_end")
+        cx = keep.tile([P, 2, HALF], F32, name="cx")
         ring = keep.tile([P, RING, 6, HALF], F32, name="ring")
 
         def transposes(tag, src32, first, count, mat):
@@ -174,8 +173,8 @@ def tile_graphconvlayer_t_kernel(tc, X, Wm, b, H, W, grad_out, out):
                 stop=stop,
             )
 
-        def column_sum(slot, fh):
-            pb = psum.tile([P, HALF], F32, tag="pb", bufs=BANKS["pb"], name="pb")
+        def column_sum(slot, fh, tag="pb"):
+            pb = psum.tile([P, HALF], F32, tag=tag, bufs=BANKS[tag], name="pb")
             mx(pb, -1, slot, fh, True, False)
             mx(pb, 0, slot, fh, False, False)
             mx(pb, 1, slot, fh, False, True)
@@ -191,7 +190,7 @@ def tile_graphconvlayer_t_kernel(tc, X, Wm, b, H, W, grad_out, out):
         quantise(grp[0], 1, GRP)
         quantise(grpx, 0, 1)
         xw = [transposes("xt", w32, 0, 2, ident), transposes("xt", w32, 2, 2, ident)]
-        move(0, GRP + 1, False)
+        move(0, 3, False)
         regroup(nc.scalar.copy, xw[0], 2, w_grp, 0)
         regroup(nc.scalar.copy, xw[1], 2, w_grp, 512)
         w_quantise(0)
@@ -199,10 +198,6 @@ def tile_graphconvlayer_t_kernel(tc, X, Wm, b, H, W, grad_out, out):
         regroup(nc.scalar.copy, xw[0], 2, w_grp, 1024)
         regroup(nc.scalar.copy, xw[1], 2, w_grp, 1536)
         w_quantise(1)
-        for fh in range(2):
-            pb = column_sum(0, fh)
-            nc.scalar.activation(out=ring[:, RING - 1, 2 + fh, :], in_=pb[:], func=COPY, scale=mask_odd[:, 0:1])
-            nc.scalar.activation(out=c_end[:, fh, :], in_=pb[:], func=COPY, scale=mask_even[:, 0:1])
 
         def unit(t, fh):
             e = t % RING
@@ -220,7 +215,11 @@ def tile_graphconvlayer_t_kernel(tc, X, Wm, b, H, W, grad_out, out):
             pa = psum.tile([P, HALF], F32, tag="pa", bufs=BANKS["pa"], name="pa")
             mx(pa, -1, t + 1, fh, True, False)
             mx(pa, 1, t + 1, fh, False, True)
-            if is_direct(t, fh):
+            if t == 0:
+                nc.vector.scalar_tensor_tensor(
+                    out=ring[:, e, fh, :], in0=cx[:, fh, :], scalar=mask_odd[:, 0:1], in1=pa[:], op0=MULT, op1=ADD)
+                nc.vector.tensor_tensor(out=ring[:, e, 2 + fh, :], in0=pa[:], in1=ring[:, ep, 4 + fh, :], op=ADD)
+            elif is_direct(t, fh):
                 nc.vector.tensor_tensor(out=ring[:, e, fh, :], in0=pa[:], in1=ring[:, ep, 2 + fh, :], op=ADD)
             else:
                 nc.vector.tensor_tensor(
@@ -237,8 +236,11 @@ def tile_graphconvlayer_t_kernel(tc, X, Wm, b, H, W, grad_out, out):
                     lo = halves[0]
                     hi = halves[-1] + 1
                     dst = ring[:, t % RING, lo:hi, :]
-                    nxt = c_end[:, lo:hi, :] if t == NT - 1 else ring[:, (t + 1) % RING, 2 + lo:2 + hi, :]
-                    engine.tensor_tensor(out=dst, in0=dst, in1=nxt, op=ADD)
+                    if t == NT - 1:
+                        engine.scalar_tensor_tensor(
+                            out=dst, in0=cx[:, lo:hi, :], scalar=mask_even[:, 0:1], in1=dst, op0=MULT, op1=ADD)
+                    else:
+                        engine.tensor_tensor(out=dst, in0=dst, in1=ring[:, (t + 1) % RING, 2 + lo:2 + hi, :], op=ADD)
 
         def store(t, n):
             e = t % RING
@@ -260,7 +262,11 @@ def tile_graphconvlayer_t_kernel(tc, X, Wm, b, H, W, grad_out, out):
                 k = starts[u]
                 g32 = g_sb[k][:].bitcast(F32)
                 xg = [transposes("xt", g32, 0, 2, perm), transposes("xt", g32, 2, 2, perm)]
+            if t == 0:
+                nc.scalar.copy(out=cx[:, u, :], in_=column_sum(0, u)[:])
             unit(t, u % 2)
+            if u == 1:
+                move(3, 2, False)
             step = u - first_unit[k] if k else 9
             if step < 2:
                 regroup(nc.scalar.copy, xg[step], 2, grp[k % 2], step * 512)

@@ -21,14 +21,14 @@ HALF = 512
 NT = 32
 GRP = 4
 NG = NT // GRP
-AHEAD = 2
 RING = 8
 STEP = 4
 FLOPS = 2 * NODES * K * FEAT
 BYTES = NODES * K * 2 + FEAT * K * 2 + NODES * FEAT * 4
 
+V_REGROUPS = (2, 4, 6)
 SHIFTS = (-1, 0, 1)
-BANKS = {"xt": 2, "pa": 4, "pb": 2}
+BANKS = {"pa": 4, "pb": 4}
 
 
 def is_direct(t, fh):
@@ -40,7 +40,7 @@ def last_add(t, fh):
         return "v"
     if t >= NT - 5:
         return "p" if is_direct(t + 1, fh) else "v"
-    if fh == 1 and t % 6 == 1:
+    if fh == 1 and t % 3 == 1:
         return "p"
     return "g"
 
@@ -105,9 +105,8 @@ def tile_graphconvlayer_t_kernel(tc, X, Wm, b, H, W, grad_out, out):
         nc.vector.tensor_reduce(out=mask_even[:], in_=id_pairs[:, :, 0], axis=mybir.AxisListType.X, op=ADD)
         nc.vector.tensor_reduce(out=mask_odd[:], in_=id_pairs[:, :, 1], axis=mybir.AxisListType.X, op=ADD)
 
-        grp = [keep.tile([P, GRP * P * 4], BF16, name="grp%d" % bb, align_bytes=64) for bb in range(2)]
+        stage = keep.tile([P, 4 * GRP * P * 4], BF16, name="stage", align_bytes=64)
         grpx = keep.tile([P, P * 4], BF16, name="grpx", align_bytes=64)
-        w_grp = keep.tile([P, FEAT * 4], BF16, name="w_grp", align_bytes=64)
         w_codes = keep.tile([P, FEAT], U32, name="w_codes", align_bytes=64)
         w_scales = keep.tile([P, FEAT], U8, name="w_scales", align_bytes=64)
         cx = keep.tile([P, 2, HALF], F32, name="cx")
@@ -131,14 +130,14 @@ def tile_graphconvlayer_t_kernel(tc, X, Wm, b, H, W, grad_out, out):
             nc.vector.quantize_mx(
                 out=w_codes[:, h * 512:(h + 1) * 512].bitcast(E4X4),
                 scales=w_scales[:, h * 512:(h + 1) * 512],
-                in_=w_grp[:, h * 2048:(h + 1) * 2048],
+                in_=stage[:, (2 + h) * 2048:(3 + h) * 2048],
             )
 
-        def quantise(src, slot0, ntile):
+        def quantise(src, col0, slot0, ntile):
             nc.vector.quantize_mx(
                 out=codes[0][:, slot0 * P:(slot0 + ntile) * P].bitcast(E5X4),
                 scales=scales[0][:, slot0 * P:(slot0 + ntile) * P],
-                in_=src[:, 0:ntile * P * 4],
+                in_=src[:, col0:col0 + ntile * P * 4],
             )
 
         def move(slot0, ntile, by_dma):
@@ -184,20 +183,28 @@ def tile_graphconvlayer_t_kernel(tc, X, Wm, b, H, W, grad_out, out):
         g32 = g_sb[0][:].bitcast(F32)
         xg = [transposes("pa", g32, 0, 2, perm), transposes("pa", g32, 2, 2, perm)]
         xx = transposes("pa", gx_sb[:].bitcast(F32), 0, 1, perm)
-        regroup(nc.scalar.copy, xg[0], 2, grp[0], 0)
-        regroup(nc.vector.tensor_copy, xg[1], 2, grp[0], 512)
+        regroup(nc.scalar.copy, xg[0], 2, stage, 0)
+        regroup(nc.vector.tensor_copy, xg[1], 2, stage, 512)
         regroup(nc.scalar.copy, xx, 1, grpx, 0)
-        quantise(grp[0], 1, GRP)
-        quantise(grpx, 0, 1)
-        xw = [transposes("xt", w32, 0, 2, ident), transposes("xt", w32, 2, 2, ident)]
-        move(0, 3, False)
-        regroup(nc.scalar.copy, xw[0], 2, w_grp, 0)
-        regroup(nc.scalar.copy, xw[1], 2, w_grp, 512)
+        quantise(stage, 0, 1, GRP)
+        quantise(grpx, 0, 0, 1)
+        xw = [transposes("pb", w32, 0, 2, ident), transposes("pb", w32, 2, 2, ident)]
+        move(0, GRP + 1, False)
+        regroup(nc.scalar.copy, xw[0], 2, stage, 2048)
+        regroup(nc.scalar.copy, xw[1], 2, stage, 2560)
         w_quantise(0)
         xw = [transposes("pb", w32, 4, 2, ident), transposes("pb", w32, 6, 2, ident)]
-        regroup(nc.scalar.copy, xw[0], 2, w_grp, 1024)
-        regroup(nc.scalar.copy, xw[1], 2, w_grp, 1536)
+        regroup(nc.scalar.copy, xw[0], 2, stage, 3072)
+        regroup(nc.scalar.copy, xw[1], 2, stage, 3584)
         w_quantise(1)
+        for k in range(1, NG):
+            g32 = g_sb[k][:].bitcast(F32)
+            tag = "pa" if k % 2 == 1 else "pb"
+            xg = [transposes(tag, g32, 0, 2, perm), transposes(tag, g32, 2, 2, perm)]
+            regroup(nc.scalar.copy, xg[0], 2, stage, (k % 4) * 1024)
+            regroup(nc.vector.tensor_copy if k in V_REGROUPS else nc.scalar.copy, xg[1], 2, stage, (k % 4) * 1024 + 512)
+            quantise(stage, (k % 4) * 2048, 1 + k * GRP, GRP)
+            move(1 + k * GRP, GRP, True)
 
         def unit(t, fh):
             e = t % RING
@@ -250,29 +257,11 @@ def tile_graphconvlayer_t_kernel(tc, X, Wm, b, H, W, grad_out, out):
                     in_=ring[q:P:4, e:e + n, 0:2, :].rearrange("p a s f -> p a (s f)"),
                 )
 
-        first_unit = {1: 0, 2: GRP}
-        starts = {0: 1, GRP: 2}
-        for k in range(3, NG):
-            first_unit[k] = (k - AHEAD) * 2 * GRP
-            starts[(k - AHEAD) * 2 * GRP] = k
-        k = 0
         for u in range(2 * NT):
             t = u // 2
-            if u in starts:
-                k = starts[u]
-                g32 = g_sb[k][:].bitcast(F32)
-                xg = [transposes("xt", g32, 0, 2, perm), transposes("xt", g32, 2, 2, perm)]
             if t == 0:
                 nc.scalar.copy(out=cx[:, u, :], in_=column_sum(0, u)[:])
             unit(t, u % 2)
-            if u == 1:
-                move(3, 2, False)
-            step = u - first_unit[k] if k else 9
-            if step < 2:
-                regroup(nc.scalar.copy, xg[step], 2, grp[k % 2], step * 512)
-            if step == 2:
-                quantise(grp[k % 2], 1 + k * GRP, GRP)
-                move(1 + k * GRP, GRP, True)
             if u % 2 == 1 and t >= 1:
                 finish(t - 1)
             if u % 2 == 1 and 2 <= t <= NT - GRP and t % 2 == 0:

@@ -11,7 +11,6 @@ I32 = mybir.dt.int32
 E5X4 = mybir.dt.float8_e5m2_x4
 E4X4 = mybir.dt.float8_e4m3fn_x4
 ADD = mybir.AluOpType.add
-MULT = mybir.AluOpType.mult
 
 P = 128
 NODES = 4096
@@ -26,21 +25,21 @@ STEP = 4
 FLOPS = 2 * NODES * K * FEAT
 BYTES = NODES * K * 2 + FEAT * K * 2 + NODES * FEAT * 4
 
+ORDER = (0, NG - 1) + tuple(range(1, NG - 1))
 V_REGROUPS = (2, 4, 6)
+C_LAST_AFTER = 3
 SHIFTS = (-1, 0, 1)
 BANKS = {"pa": 4, "pb": 4}
 
 
 def is_direct(t, fh):
-    return t >= NT - 4 or (fh == 1 and t % 3 != 0)
+    return t == 0 or NT - 4 <= t <= NT - 2 or (fh == 1 and t % 3 != 0 and t < NT - 1)
 
 
 def last_add(t, fh):
-    if t == NT - 1:
-        return "v"
-    if t >= NT - 5:
-        return "p" if is_direct(t + 1, fh) else "v"
-    if fh == 1 and t % 3 == 1:
+    if t >= NT - 2:
+        return "none"
+    if t >= NT - 5 or (fh == 1 and t % 3 == 1):
         return "p"
     return "g"
 
@@ -48,9 +47,7 @@ def last_add(t, fh):
 def tile_graphconvlayer_t_kernel(tc, X, Wm, b, H, W, grad_out, out):
     nc = tc.nc
     assert H == 32 and W == 64
-    g_flat = grad_out.flatten_outer_dims()
-    g_pt = g_flat.rearrange("(p t) k -> p t k", t=NT)
-    g_mc = g_flat.rearrange("(m c) k -> m c k", c=64)
+    g_pt = grad_out.flatten_outer_dims().rearrange("(p t) k -> p t k", t=NT)
     w_pj = Wm.rearrange("(j p) k -> p j k", p=P)
     out_q = out.rearrange("i (r h t) f -> i h r t f", h=2, t=NT)
 
@@ -59,7 +56,6 @@ def tile_graphconvlayer_t_kernel(tc, X, Wm, b, H, W, grad_out, out):
         psum = ctx.enter_context(tc.psum_pool(name="psum", bufs=2))
 
         w_sb = keep.tile([P, 8 * K], BF16, name="w_sb")
-        gx_sb = keep.tile([P, K], BF16, name="gx_sb")
         g_sb = [keep.tile([P, GRP * K], BF16, name="g_sb%d" % g) for g in range(NG)]
 
         def load_w(h):
@@ -74,12 +70,11 @@ def tile_graphconvlayer_t_kernel(tc, X, Wm, b, H, W, grad_out, out):
                 in_=g_pt[:, g * GRP:(g + 1) * GRP, :],
             )
 
-        load_g(0)
-        nc.sync.dma_start(out=gx_sb[0:P:2, :], in_=g_mc[:, 32, :])
-        nc.sync.dma_start(out=gx_sb[1:P:2, :], in_=g_mc[:, 31, :])
+        load_g(ORDER[0])
+        load_g(ORDER[1])
         load_w(0)
         load_w(1)
-        for g in range(1, NG):
+        for g in ORDER[2:]:
             load_g(g)
 
         ctx.enter_context(tc.manual_schedule())
@@ -94,51 +89,40 @@ def tile_graphconvlayer_t_kernel(tc, X, Wm, b, H, W, grad_out, out):
         codes = {}
         scales = {}
         for s in SHIFTS:
-            codes[s] = keep.tile([P, (NT + 1) * P], U32, name="codes%d" % (s + 1), align_bytes=64)
-            scales[s] = keep.tile([P, (NT + 1) * P], U8, name="scales%d" % (s + 1), align_bytes=64)
+            codes[s] = keep.tile([P, NT * P], U32, name="codes%d" % (s + 1), align_bytes=64)
+            scales[s] = keep.tile([P, NT * P], U8, name="scales%d" % (s + 1), align_bytes=64)
             nc.vector.memset(scales[s][:].bitcast(I32), 0)
         nc.vector.memset(codes[1][:].bitcast(I32).rearrange("p (a c) -> p a c", c=P)[:, :, P - STEP:P], 0)
         nc.vector.memset(codes[-1][:].bitcast(I32).rearrange("p (a c) -> p a c", c=P)[:, :, 0:STEP], 0)
-        id_pairs = ident[:].rearrange("p (a e) -> p a e", e=2)
-        mask_even = keep.tile([P, 1], F32, name="mask_even")
-        mask_odd = keep.tile([P, 1], F32, name="mask_odd")
-        nc.vector.tensor_reduce(out=mask_even[:], in_=id_pairs[:, :, 0], axis=mybir.AxisListType.X, op=ADD)
-        nc.vector.tensor_reduce(out=mask_odd[:], in_=id_pairs[:, :, 1], axis=mybir.AxisListType.X, op=ADD)
 
         stage = keep.tile([P, 4 * GRP * P * 4], BF16, name="stage", align_bytes=64)
-        grpx = keep.tile([P, P * 4], BF16, name="grpx", align_bytes=64)
         w_codes = keep.tile([P, FEAT], U32, name="w_codes", align_bytes=64)
         w_scales = keep.tile([P, FEAT], U8, name="w_scales", align_bytes=64)
-        cx = keep.tile([P, 2, HALF], F32, name="cx")
+        c_last = keep.tile([P, 2, HALF], F32, name="c_last")
+        c_right = keep.tile([P, 2, HALF], F32, name="c_right")
         ring = keep.tile([P, RING, 6, HALF], F32, name="ring")
+        nc.gpsimd.memset(ring[:, RING - 1, 2:4, :], 0.0)
+        nc.gpsimd.memset(c_right[:], 0.0)
 
-        def transposes(tag, src32, first, count, mat):
+        def transposes(tag, src32, first, mat):
             xt = psum.tile([P, 2, 256], F32, tag=tag, bufs=BANKS[tag], name="xt")
-            for jj in range(count):
+            for jj in range(2):
                 for u in range(2):
                     lo = (first + jj) * 256 + u * P
                     nc.tensor.transpose(xt[:, u, jj * P:(jj + 1) * P], src32[:, lo:lo + P], mat[:])
             return xt
 
-        def regroup(engine, xt, ntile, dst, word0):
+        def regroup(engine, xt, word0):
             engine(
-                out=dst[:].bitcast(F32)[:, word0:word0 + ntile * 256].rearrange("p (n u) -> p n u", u=2),
-                in_=xt[:, :, 0:ntile * P].rearrange("p u n -> p n u"),
+                out=stage[:].bitcast(F32)[:, word0:word0 + 512].rearrange("p (n u) -> p n u", u=2),
+                in_=xt[:].rearrange("p u n -> p n u"),
             )
 
-        def w_quantise(h):
-            nc.vector.quantize_mx(
-                out=w_codes[:, h * 512:(h + 1) * 512].bitcast(E4X4),
-                scales=w_scales[:, h * 512:(h + 1) * 512],
-                in_=stage[:, (2 + h) * 2048:(3 + h) * 2048],
-            )
-
-        def quantise(src, col0, slot0, ntile):
-            nc.vector.quantize_mx(
-                out=codes[0][:, slot0 * P:(slot0 + ntile) * P].bitcast(E5X4),
-                scales=scales[0][:, slot0 * P:(slot0 + ntile) * P],
-                in_=src[:, col0:col0 + ntile * P * 4],
-            )
+        def stage_in(src, first, buf, tag, mat, second_engine):
+            src32 = src[:].bitcast(F32)
+            xt = [transposes(tag, src32, first, mat), transposes(tag, src32, first + 2, mat)]
+            regroup(nc.scalar.copy, xt[0], buf * 1024)
+            regroup(second_engine, xt[1], buf * 1024 + 512)
 
         def move(slot0, ntile, by_dma):
             lo = slot0 * P
@@ -161,72 +145,84 @@ def tile_graphconvlayer_t_kernel(tc, X, Wm, b, H, W, grad_out, out):
                 else:
                     nc.vector.tensor_copy(out=dst, in_=src)
 
-        def mx(acc, s, slot, fh, start, stop):
+        def prepare_group(k, buf, tag):
+            stage_in(g_sb[k], 0, buf, tag, perm, nc.vector.tensor_copy if k in V_REGROUPS else nc.scalar.copy)
+            nc.vector.quantize_mx(
+                out=codes[0][:, k * GRP * P:(k + 1) * GRP * P].bitcast(E5X4),
+                scales=scales[0][:, k * GRP * P:(k + 1) * GRP * P],
+                in_=stage[:, buf * 2048:(buf + 1) * 2048],
+            )
+
+        def prepare_w(h, buf):
+            stage_in(w_sb, 4 * h, buf, "pb", ident, nc.scalar.copy)
+            nc.vector.quantize_mx(
+                out=w_codes[:, h * 512:(h + 1) * 512].bitcast(E4X4),
+                scales=w_scales[:, h * 512:(h + 1) * 512],
+                in_=stage[:, buf * 2048:(buf + 1) * 2048],
+            )
+
+        def mx(acc, s, t, fh, start, stop):
             nc.tensor.matmul_mx(
                 out=acc[:],
-                lhsT=codes[s][:, slot * P:(slot + 1) * P].bitcast(E5X4),
-                lhsT_scale=scales[s][:, slot * P:(slot + 1) * P],
+                lhsT=codes[s][:, t * P:(t + 1) * P].bitcast(E5X4),
+                lhsT_scale=scales[s][:, t * P:(t + 1) * P],
                 rhs=w_codes[:, fh * 512:(fh + 1) * 512].bitcast(E4X4),
                 rhs_scale=w_scales[:, fh * 512:(fh + 1) * 512],
                 start=start,
                 stop=stop,
             )
 
-        def column_sum(slot, fh, tag="pb"):
-            pb = psum.tile([P, HALF], F32, tag=tag, bufs=BANKS[tag], name="pb")
-            mx(pb, -1, slot, fh, True, False)
-            mx(pb, 0, slot, fh, False, False)
-            mx(pb, 1, slot, fh, False, True)
+        def column_sum(t, fh):
+            pb = psum.tile([P, HALF], F32, tag="pb", bufs=BANKS["pb"], name="pb")
+            mx(pb, -1, t, fh, True, False)
+            mx(pb, 0, t, fh, False, False)
+            mx(pb, 1, t, fh, False, True)
             return pb
 
-        w32 = w_sb[:].bitcast(F32)
-        g32 = g_sb[0][:].bitcast(F32)
-        xg = [transposes("pa", g32, 0, 2, perm), transposes("pa", g32, 2, 2, perm)]
-        xx = transposes("pa", gx_sb[:].bitcast(F32), 0, 1, perm)
-        regroup(nc.scalar.copy, xg[0], 2, stage, 0)
-        regroup(nc.vector.tensor_copy, xg[1], 2, stage, 512)
-        regroup(nc.scalar.copy, xx, 1, grpx, 0)
-        quantise(stage, 0, 1, GRP)
-        quantise(grpx, 0, 0, 1)
-        xw = [transposes("pb", w32, 0, 2, ident), transposes("pb", w32, 2, 2, ident)]
-        move(0, GRP + 1, False)
-        regroup(nc.scalar.copy, xw[0], 2, stage, 2048)
-        regroup(nc.scalar.copy, xw[1], 2, stage, 2560)
-        w_quantise(0)
-        xw = [transposes("pb", w32, 4, 2, ident), transposes("pb", w32, 6, 2, ident)]
-        regroup(nc.scalar.copy, xw[0], 2, stage, 3072)
-        regroup(nc.scalar.copy, xw[1], 2, stage, 3584)
-        w_quantise(1)
-        for k in range(1, NG):
-            g32 = g_sb[k][:].bitcast(F32)
-            tag = "pa" if k % 2 == 1 else "pb"
-            xg = [transposes(tag, g32, 0, 2, perm), transposes(tag, g32, 2, 2, perm)]
-            regroup(nc.scalar.copy, xg[0], 2, stage, (k % 4) * 1024)
-            regroup(nc.vector.tensor_copy if k in V_REGROUPS else nc.scalar.copy, xg[1], 2, stage, (k % 4) * 1024 + 512)
-            quantise(stage, (k % 4) * 2048, 1 + k * GRP, GRP)
-            move(1 + k * GRP, GRP, True)
+        prepare_group(0, 0, "pa")
+        move(0, GRP, False)
+        prepare_group(NG - 1, 1, "pa")
+        move(NT - 1, 1, False)
+        prepare_w(0, 2)
+        prepare_w(1, 3)
+        for j in range(2, NG):
+            k = ORDER[j]
+            prepare_group(k, (j + 2) % 4, "pa" if j % 2 == 0 else "pb")
+            if j == C_LAST_AFTER:
+                for fh in range(2):
+                    nc.scalar.copy(out=c_last[:, fh, :], in_=column_sum(NT - 1, fh)[:])
+                nc.sync.dma_start(out=ring[1:P:2, RING - 1, 2:4, :], in_=c_last[0:P:2, :, :])
+                for jj in range(2, j):
+                    move(ORDER[jj] * GRP, GRP, True)
+            if j >= C_LAST_AFTER:
+                move(k * GRP, GRP, True)
+        move(NT - GRP, GRP - 1, True)
 
-        def unit(t, fh):
+        def first_part(t, fh):
             e = t % RING
             ep = (t - 1) % RING
             if is_direct(t, fh):
-                pb = column_sum(t + 1, fh)
-                if t < NT - 1:
+                pb = column_sum(t, fh)
+                if t == NT - 3:
+                    nc.vector.tensor_tensor(out=ring[:, e, 2 + fh, :], in0=pb[:], in1=c_last[:, fh, :], op=ADD)
+                elif t == NT - 2:
+                    nc.vector.tensor_tensor(out=ring[:, e, 2 + fh, :], in0=pb[:], in1=c_right[:, fh, :], op=ADD)
+                else:
                     nc.scalar.copy(out=ring[:, e, 2 + fh, :], in_=pb[:])
-                if t >= 1 and last_add(t - 1, fh) == "p":
+                if t > 0 and last_add(t - 1, fh) == "p":
                     nc.vector.tensor_tensor(out=ring[:, ep, fh, :], in0=pb[:], in1=ring[:, ep, fh, :], op=ADD)
-            else:
+            elif t < NT - 1:
                 pb = psum.tile([P, HALF], F32, tag="pb", bufs=BANKS["pb"], name="pb")
-                mx(pb, 0, t + 1, fh, True, True)
+                mx(pb, 0, t, fh, True, True)
                 nc.scalar.copy(out=ring[:, ep, 4 + fh, :], in_=pb[:])
+
+        def second_part(t, fh):
+            e = t % RING
+            ep = (t - 1) % RING
             pa = psum.tile([P, HALF], F32, tag="pa", bufs=BANKS["pa"], name="pa")
-            mx(pa, -1, t + 1, fh, True, False)
-            mx(pa, 1, t + 1, fh, False, True)
-            if t == 0:
-                nc.vector.scalar_tensor_tensor(
-                    out=ring[:, e, fh, :], in0=cx[:, fh, :], scalar=mask_odd[:, 0:1], in1=pa[:], op0=MULT, op1=ADD)
-                nc.vector.tensor_tensor(out=ring[:, e, 2 + fh, :], in0=pa[:], in1=ring[:, ep, 4 + fh, :], op=ADD)
-            elif is_direct(t, fh):
+            mx(pa, -1, t, fh, True, False)
+            mx(pa, 1, t, fh, False, True)
+            if is_direct(t, fh) or t == NT - 1:
                 nc.vector.tensor_tensor(out=ring[:, e, fh, :], in0=pa[:], in1=ring[:, ep, 2 + fh, :], op=ADD)
             else:
                 nc.vector.tensor_tensor(
@@ -237,17 +233,12 @@ def tile_graphconvlayer_t_kernel(tc, X, Wm, b, H, W, grad_out, out):
                 )
 
         def finish(t):
-            for how, engine in (("g", nc.gpsimd), ("v", nc.vector)):
-                halves = [fh for fh in range(2) if last_add(t, fh) == how]
-                if halves:
-                    lo = halves[0]
-                    hi = halves[-1] + 1
-                    dst = ring[:, t % RING, lo:hi, :]
-                    if t == NT - 1:
-                        engine.scalar_tensor_tensor(
-                            out=dst, in0=cx[:, lo:hi, :], scalar=mask_even[:, 0:1], in1=dst, op0=MULT, op1=ADD)
-                    else:
-                        engine.tensor_tensor(out=dst, in0=dst, in1=ring[:, (t + 1) % RING, 2 + lo:2 + hi, :], op=ADD)
+            halves = [fh for fh in range(2) if last_add(t, fh) == "g"]
+            if halves:
+                lo = halves[0]
+                hi = halves[-1] + 1
+                dst = ring[:, t % RING, lo:hi, :]
+                nc.gpsimd.tensor_tensor(out=dst, in0=dst, in1=ring[:, (t + 1) % RING, 2 + lo:2 + hi, :], op=ADD)
 
         def store(t, n):
             e = t % RING
@@ -257,16 +248,22 @@ def tile_graphconvlayer_t_kernel(tc, X, Wm, b, H, W, grad_out, out):
                     in_=ring[q:P:4, e:e + n, 0:2, :].rearrange("p a s f -> p a (s f)"),
                 )
 
-        for u in range(2 * NT):
-            t = u // 2
+        for t in range(NT):
+            for fh in range(2):
+                first_part(t, fh)
+                if t > 0:
+                    second_part(t, fh)
             if t == 0:
-                nc.scalar.copy(out=cx[:, u, :], in_=column_sum(0, u)[:])
-            unit(t, u % 2)
-            if u % 2 == 1 and t >= 1:
+                nc.sync.dma_start(out=c_right[0:P:2, :, :], in_=ring[1:P:2, 0, 2:4, :])
+            if t == 1:
+                second_part(0, 0)
+                second_part(0, 1)
+            if t >= 1:
                 finish(t - 1)
-            if u % 2 == 1 and 2 <= t <= NT - GRP and t % 2 == 0:
+            if 2 <= t <= NT - GRP and t % 2 == 0:
                 store(t - 2, 2)
-            if u % 2 == 1 and t > NT - GRP:
+            if t == NT - 3:
                 store(t - 1, 1)
-        finish(NT - 1)
+            if t == NT - 2:
+                store(t - 1, 2)
         store(NT - 1, 1)

@@ -249,10 +249,17 @@ def tile_graphconvlayer_t_kernel(tc, X, Wm, b, H, W, grad_out, out):
                 )
 
         for t in range(NT):
-            for fh in range(2):
-                first_part(t, fh)
-                if t > 0:
-                    second_part(t, fh)
+            if t == NT - 2:
+                first_part(t, 0)
+                first_part(t, 1)
+                store(t - 1, 1)
+                second_part(t, 0)
+                second_part(t, 1)
+            else:
+                for fh in range(2):
+                    first_part(t, fh)
+                    if t > 0:
+                        second_part(t, fh)
             if t == 0:
                 nc.sync.dma_start(out=c_right[0:P:2, :, :], in_=ring[1:P:2, 0, 2:4, :])
             if t == 1:
@@ -265,5 +272,5 @@ def tile_graphconvlayer_t_kernel(tc, X, Wm, b, H, W, grad_out, out):
             if t == NT - 3:
                 store(t - 1, 1)
             if t == NT - 2:
-                store(t - 1, 2)
+                store(t, 1)
         store(NT - 1, 1)

@@ -27,6 +27,7 @@ BYTES = NODES * K * 2 + FEAT * K * 2 + NODES * FEAT * 4
 
 ORDER = (0, NG - 1) + tuple(range(1, NG - 1))
 V_REGROUPS = (2, 4, 6)
+LATE = 3
 C_LAST_AFTER = 3
 SHIFTS = (-1, 0, 1)
 BANKS = {"pa": 4, "pb": 4}
@@ -185,7 +186,7 @@ def tile_graphconvlayer_t_kernel(tc, X, Wm, b, H, W, grad_out, out):
         move(NT - 1, 1, False)
         prepare_w(0, 2)
         prepare_w(1, 3)
-        for j in range(2, NG):
+        def next_group(j):
             k = ORDER[j]
             prepare_group(k, (j + 2) % 4, "pa" if j % 2 == 0 else "pb")
             if j == C_LAST_AFTER:
@@ -196,7 +197,9 @@ def tile_graphconvlayer_t_kernel(tc, X, Wm, b, H, W, grad_out, out):
                     move(ORDER[jj] * GRP, GRP, True)
             if j >= C_LAST_AFTER:
                 move(k * GRP, GRP, True)
-        move(NT - GRP, GRP - 1, True)
+
+        for j in range(2, NG - LATE):
+            next_group(j)
 
         def first_part(t, fh):
             e = t % RING
@@ -260,8 +263,12 @@ def tile_graphconvlayer_t_kernel(tc, X, Wm, b, H, W, grad_out, out):
                     first_part(t, fh)
                     if t > 0:
                         second_part(t, fh)
+                    if 2 * t + fh - 1 in range(LATE):
+                        next_group(NG - LATE + 2 * t + fh - 1)
             if t == 0:
                 nc.sync.dma_start(out=c_right[0:P:2, :, :], in_=ring[1:P:2, 0, 2:4, :])
+            if t == 2:
+                move(NT - GRP, GRP - 1, True)
             if t == 1:
                 second_part(0, 0)
                 second_part(0, 1)

@@ -20,7 +20,9 @@ HALF = 512
 NT = 32
 GRP = 4
 NG = NT // GRP
-RING = 8
+ND = 14
+NC = 6
+NB = 4
 STEP = 4
 FLOPS = 2 * NODES * K * FEAT
 BYTES = NODES * K * 2 + FEAT * K * 2 + NODES * FEAT * 4
@@ -101,8 +103,18 @@ def tile_graphconvlayer_t_kernel(tc, X, Wm, b, H, W, grad_out, out):
         w_scales = keep.tile([P, FEAT], U8, name="w_scales", align_bytes=64)
         c_last = keep.tile([P, 2, HALF], F32, name="c_last")
         c_right = keep.tile([P, 2, HALF], F32, name="c_right")
-        ring = keep.tile([P, RING, 6, HALF], F32, name="ring")
-        nc.gpsimd.memset(ring[:, RING - 1, 2:4, :], 0.0)
+        work = keep.tile([P, 2 * (ND + NC + NB), HALF], F32, name="work")
+
+        def d_at(t, fh):
+            return 2 * (t % ND) + fh
+
+        def c_at(t, fh):
+            return 2 * ND + 2 * (t % NC) + fh
+
+        def b_at(t, fh):
+            return 2 * (ND + NC) + 2 * (t % NB) + fh
+
+        nc.gpsimd.memset(work[:, c_at(-1, 0):c_at(-1, 0) + 2, :], 0.0)
         nc.gpsimd.memset(c_right[:], 0.0)
 
         def transposes(tag, src32, first, mat):
@@ -192,7 +204,7 @@ def tile_graphconvlayer_t_kernel(tc, X, Wm, b, H, W, grad_out, out):
             if j == C_LAST_AFTER:
                 for fh in range(2):
                     nc.scalar.copy(out=c_last[:, fh, :], in_=column_sum(NT - 1, fh)[:])
-                nc.sync.dma_start(out=ring[1:P:2, RING - 1, 2:4, :], in_=c_last[0:P:2, :, :])
+                nc.sync.dma_start(out=work[1:P:2, c_at(-1, 0):c_at(-1, 0) + 2, :], in_=c_last[0:P:2, :, :])
                 for jj in range(2, j):
                     move(ORDER[jj] * GRP, GRP, True)
             if j >= C_LAST_AFTER:
@@ -202,36 +214,32 @@ def tile_graphconvlayer_t_kernel(tc, X, Wm, b, H, W, grad_out, out):
             next_group(j)
 
         def first_part(t, fh):
-            e = t % RING
-            ep = (t - 1) % RING
             if is_direct(t, fh):
                 pb = column_sum(t, fh)
                 if t == NT - 3:
-                    nc.vector.tensor_tensor(out=ring[:, e, 2 + fh, :], in0=pb[:], in1=c_last[:, fh, :], op=ADD)
+                    nc.vector.tensor_tensor(out=work[:, c_at(t, fh), :], in0=pb[:], in1=c_last[:, fh, :], op=ADD)
                 elif t == NT - 2:
-                    nc.vector.tensor_tensor(out=ring[:, e, 2 + fh, :], in0=pb[:], in1=c_right[:, fh, :], op=ADD)
+                    nc.vector.tensor_tensor(out=work[:, c_at(t, fh), :], in0=pb[:], in1=c_right[:, fh, :], op=ADD)
                 else:
-                    nc.scalar.copy(out=ring[:, e, 2 + fh, :], in_=pb[:])
+                    nc.scalar.copy(out=work[:, c_at(t, fh), :], in_=pb[:])
                 if t > 0 and last_add(t - 1, fh) == "p":
-                    nc.vector.tensor_tensor(out=ring[:, ep, fh, :], in0=pb[:], in1=ring[:, ep, fh, :], op=ADD)
+                    nc.vector.tensor_tensor(out=work[:, d_at(t - 1, fh), :], in0=pb[:], in1=work[:, d_at(t - 1, fh), :], op=ADD)
             elif t < NT - 1:
                 pb = psum.tile([P, HALF], F32, tag="pb", bufs=BANKS["pb"], name="pb")
                 mx(pb, 0, t, fh, True, True)
-                nc.scalar.copy(out=ring[:, ep, 4 + fh, :], in_=pb[:])
+                nc.scalar.copy(out=work[:, b_at(t, fh), :], in_=pb[:])
 
         def second_part(t, fh):
-            e = t % RING
-            ep = (t - 1) % RING
             pa = psum.tile([P, HALF], F32, tag="pa", bufs=BANKS["pa"], name="pa")
             mx(pa, -1, t, fh, True, False)
             mx(pa, 1, t, fh, False, True)
             if is_direct(t, fh) or t == NT - 1:
-                nc.vector.tensor_tensor(out=ring[:, e, fh, :], in0=pa[:], in1=ring[:, ep, 2 + fh, :], op=ADD)
+                nc.vector.tensor_tensor(out=work[:, d_at(t, fh), :], in0=pa[:], in1=work[:, c_at(t - 1, fh), :], op=ADD)
             else:
                 nc.vector.tensor_tensor(
-                    out=ring[:, e, fh:fh + 3:2, :],
+                    out=work[:, d_at(t, fh):c_at(t, fh) + 1:c_at(t, fh) - d_at(t, fh), :],
                     in0=pa[:].unsqueeze(1).to_broadcast([P, 2, HALF]),
-                    in1=ring[:, ep, 2 + fh:2 + fh + 3:2, :],
+                    in1=work[:, c_at(t - 1, fh):b_at(t, fh) + 1:b_at(t, fh) - c_at(t - 1, fh), :],
                     op=ADD,
                 )
 
@@ -240,15 +248,14 @@ def tile_graphconvlayer_t_kernel(tc, X, Wm, b, H, W, grad_out, out):
             if halves:
                 lo = halves[0]
                 hi = halves[-1] + 1
-                dst = ring[:, t % RING, lo:hi, :]
-                nc.gpsimd.tensor_tensor(out=dst, in0=dst, in1=ring[:, (t + 1) % RING, 2 + lo:2 + hi, :], op=ADD)
+                dst = work[:, d_at(t, lo):d_at(t, lo) + hi - lo, :]
+                nc.gpsimd.tensor_tensor(out=dst, in0=dst, in1=work[:, c_at(t + 1, lo):c_at(t + 1, lo) + hi - lo, :], op=ADD)
 
         def store(t, n):
-            e = t % RING
             for q in range(4):
                 nc.sync.dma_start(
                     out=out_q[q // 2, q % 2, :, t:t + n, :],
-                    in_=ring[q:P:4, e:e + n, 0:2, :].rearrange("p a s f -> p a (s f)"),
+                    in_=work[q:P:4, d_at(t, 0):d_at(t, 0) + 2 * n, :].rearrange("p (a v) f -> p a (v f)", v=2),
                 )
 
         for t in range(NT):
@@ -266,7 +273,7 @@ def tile_graphconvlayer_t_kernel(tc, X, Wm, b, H, W, grad_out, out):
                     if 2 * t + fh - 1 in range(LATE):
                         next_group(NG - LATE + 2 * t + fh - 1)
             if t == 0:
-                nc.sync.dma_start(out=c_right[0:P:2, :, :], in_=ring[1:P:2, 0, 2:4, :])
+                nc.sync.dma_start(out=c_right[0:P:2, :, :], in_=work[1:P:2, c_at(0, 0):c_at(0, 0) + 2, :])
             if t == 2:
                 move(NT - GRP, GRP - 1, True)
             if t == 1:

@@ -36,7 +36,7 @@ BANKS = {"pa": 4, "pb": 4}
 
 
 def is_direct(t, fh):
-    return t == 0 or NT - 4 <= t <= NT - 2 or (fh == 1 and t % 3 != 0 and t < NT - 1)
+    return t == 0 or NT - 4 <= t <= NT - 2 or (fh == 1 and t % 3 != 0 and t % 6 != 1 and t < NT - 1)
 
 
 def last_add(t, fh):

@@ -82,6 +82,15 @@ def tile_graphconvlayer_t_kernel(tc, X, Wm, b, H, W, grad_out, out):
 
         ctx.enter_context(tc.manual_schedule())
 
+        zeros = keep.tile([P, HALF], BF16, name="zeros")
+        nc.vector.memset(zeros[:], 0.0)
+
+        def keep_busy(tag, n):
+            idle = psum.tile([P, HALF], F32, tag=tag, bufs=BANKS[tag], name="idle")
+            for i in range(n):
+                nc.tensor.matmul(idle[:], lhsT=zeros[:, 0:P], rhs=zeros[:], start=True, stop=True)
+
+        keep_busy("pb", 10)
         ident = keep.tile([P, P], F32, name="ident")
         make_identity(nc, ident[:])
         perm = keep.tile([P, P], F32, name="perm")
@@ -193,14 +202,20 @@ def tile_graphconvlayer_t_kernel(tc, X, Wm, b, H, W, grad_out, out):
             return pb
 
         prepare_group(0, 0, "pa")
+        keep_busy("pb", 2)
         move(0, GRP, False)
         prepare_group(NG - 1, 1, "pa")
+        keep_busy("pb", 2)
         move(NT - 1, 1, False)
         prepare_w(0, 2)
+        keep_busy("pa", 2)
         prepare_w(1, 3)
+        keep_busy("pa", 2)
         def next_group(j):
             k = ORDER[j]
             prepare_group(k, (j + 2) % 4, "pa" if j % 2 == 0 else "pb")
+            if j == 2:
+                keep_busy("pb", 2)
             if j == C_LAST_AFTER:
                 for fh in range(2):
                     nc.scalar.copy(out=c_last[:, fh, :], in_=column_sum(NT - 1, fh)[:])

@@ -27,24 +27,26 @@ STEP = 4
 FLOPS = 2 * NODES * K * FEAT
 BYTES = NODES * K * 2 + FEAT * K * 2 + NODES * FEAT * 4
 
-ORDER = (0, NG - 1) + tuple(range(1, NG - 1))
-V_REGROUPS = (2, 4, 6)
-LATE = 3
-C_LAST_AFTER = 3
+SEQ = (31, 30, 29, 28) + tuple(range(27))
+GROUPS = (7,) + tuple(range(7))
 SHIFTS = (-1, 0, 1)
 BANKS = {"pa": 4, "pb": 4}
+EARLY = 1
+G_FROM = 6
+A27_AT = 16
+ZERO_AFTER = 8
+VMOVE = 1
+VREG = (0, )
 
 
 def is_direct(t, fh):
-    return t == 0 or NT - 4 <= t <= NT - 2 or (fh == 1 and t % 3 != 0 and t % 6 != 1 and t < NT - 1)
+    return t in (24, 25, 26) or (fh == 1 and t < 24 and t % 3 != 0 and t % 9 != 7)
 
 
 def last_add(t, fh):
-    if t >= NT - 2:
-        return "none"
-    if t >= NT - 5 or (fh == 1 and t % 3 == 1):
+    if t in (24, 25) or (t < 24 and fh == 1 and (t % 3 == 1 or t in (12, 21))) or (t == 23 and fh == 0):
         return "p"
-    return "g"
+    return "none" if t == 26 else "g"
 
 
 def tile_graphconvlayer_t_kernel(tc, X, Wm, b, H, W, grad_out, out):
@@ -73,11 +75,10 @@ def tile_graphconvlayer_t_kernel(tc, X, Wm, b, H, W, grad_out, out):
                 in_=g_pt[:, g * GRP:(g + 1) * GRP, :],
             )
 
-        load_g(ORDER[0])
-        load_g(ORDER[1])
+        load_g(GROUPS[0])
         load_w(0)
         load_w(1)
-        for g in ORDER[2:]:
+        for g in GROUPS[1:]:
             load_g(g)
 
         ctx.enter_context(tc.manual_schedule())
@@ -90,7 +91,6 @@ def tile_graphconvlayer_t_kernel(tc, X, Wm, b, H, W, grad_out, out):
             for i in range(n):
                 nc.tensor.matmul(idle[:], lhsT=zeros[:, 0:P], rhs=zeros[:], start=True, stop=True)
 
-        keep_busy("pb", 10)
         ident = keep.tile([P, P], F32, name="ident")
         make_identity(nc, ident[:])
         perm = keep.tile([P, P], F32, name="perm")
@@ -110,20 +110,32 @@ def tile_graphconvlayer_t_kernel(tc, X, Wm, b, H, W, grad_out, out):
         stage = keep.tile([P, 4 * GRP * P * 4], BF16, name="stage", align_bytes=64)
         w_codes = keep.tile([P, FEAT], U32, name="w_codes", align_bytes=64)
         w_scales = keep.tile([P, FEAT], U8, name="w_scales", align_bytes=64)
-        c_last = keep.tile([P, 2, HALF], F32, name="c_last")
         c_right = keep.tile([P, 2, HALF], F32, name="c_right")
-        work = keep.tile([P, 2 * (ND + NC + NB), HALF], F32, name="work")
+        work = keep.tile([P, 2 * (ND + NC + NB + 2), HALF], F32, name="work")
+        D_28 = 2 * (ND + NC + NB)
+        C_28 = D_28 + 2
 
         def d_at(t, fh):
-            return 2 * (t % ND) + fh
+            if t == 28:
+                return D_28 + fh
+            if t == 27:
+                return C_28 + fh
+            return 2 * ((t + 4 if t < 27 else t - 28) % ND) + fh
+
+        def c_ring(s, fh):
+            return 2 * ND + 2 * (s % NC) + fh
 
         def c_at(t, fh):
-            return 2 * ND + 2 * (t % NC) + fh
+            return C_28 + fh if t == 28 else c_ring(SEQ.index(t), fh)
+
+        def c_before(t, fh):
+            return c_ring(SEQ.index(t) - 1, fh)
 
         def b_at(t, fh):
-            return 2 * (ND + NC) + 2 * (t % NB) + fh
+            return 2 * (ND + NC) + 2 * (SEQ.index(t) % NB) + fh
 
-        nc.gpsimd.memset(work[:, c_at(-1, 0):c_at(-1, 0) + 2, :], 0.0)
+        C_LEFT = c_ring(3, 0)
+        nc.gpsimd.memset(work[:, C_LEFT:C_LEFT + 2, :], 0.0)
         nc.gpsimd.memset(c_right[:], 0.0)
 
         def transposes(tag, src32, first, mat):
@@ -146,7 +158,7 @@ def tile_graphconvlayer_t_kernel(tc, X, Wm, b, H, W, grad_out, out):
             regroup(nc.scalar.copy, xt[0], buf * 1024)
             regroup(second_engine, xt[1], buf * 1024 + 512)
 
-        def move(slot0, ntile, by_dma):
+        def move(slot0, ntile, by_dma, scale_engine=None):
             lo = slot0 * P
             hi = (slot0 + ntile) * P
             mid = codes[0][:].bitcast(I32)[:, lo:hi].rearrange("p (a c) -> p a c", c=P)
@@ -164,19 +176,38 @@ def tile_graphconvlayer_t_kernel(tc, X, Wm, b, H, W, grad_out, out):
             for dst, src in pairs:
                 if by_dma:
                     nc.sync.dma_start(out=dst, in_=src)
+                elif scale_engine is not None and len(dst.shape) == 2:
+                    scale_engine.tensor_copy(out=dst, in_=src)
                 else:
                     nc.vector.tensor_copy(out=dst, in_=src)
 
-        def prepare_group(k, buf, tag):
-            stage_in(g_sb[k], 0, buf, tag, perm, nc.vector.tensor_copy if k in V_REGROUPS else nc.scalar.copy)
+        def stage_group(j):
+            stage_in(g_sb[GROUPS[j]], 0, j % 4, "pb", perm, nc.vector.tensor_copy if j in VREG else nc.scalar.copy)
+
+        def quantise_group(j):
+            buf = j % 4
+            k = GROUPS[j]
             nc.vector.quantize_mx(
                 out=codes[0][:, k * GRP * P:(k + 1) * GRP * P].bitcast(E5X4),
                 scales=scales[0][:, k * GRP * P:(k + 1) * GRP * P],
                 in_=stage[:, buf * 2048:(buf + 1) * 2048],
             )
 
-        def prepare_w(h, buf):
-            stage_in(w_sb, 4 * h, buf, "pb", ident, nc.scalar.copy)
+        def move_group(j):
+            k = GROUPS[j]
+            if j == NG - 1:
+                move(k * GRP + 3, 1, False, nc.gpsimd)
+                move(k * GRP, GRP - 1, True)
+            elif j < VMOVE:
+                move(k * GRP, GRP, False)
+            else:
+                move(k * GRP, GRP, True)
+
+        def stage_w(h):
+            stage_in(w_sb, 4 * h, 2 + h, "pa", ident, nc.scalar.copy)
+
+        def quantise_w(h):
+            buf = 2 + h
             nc.vector.quantize_mx(
                 out=w_codes[:, h * 512:(h + 1) * 512].bitcast(E4X4),
                 scales=w_scales[:, h * 512:(h + 1) * 512],
@@ -201,60 +232,46 @@ def tile_graphconvlayer_t_kernel(tc, X, Wm, b, H, W, grad_out, out):
             mx(pb, 1, t, fh, False, True)
             return pb
 
-        prepare_group(0, 0, "pa")
-        keep_busy("pb", 2)
-        move(0, GRP, False)
-        prepare_group(NG - 1, 1, "pa")
-        keep_busy("pb", 2)
-        move(NT - 1, 1, False)
-        prepare_w(0, 2)
-        keep_busy("pa", 2)
-        prepare_w(1, 3)
-        keep_busy("pa", 2)
-        def next_group(j):
-            k = ORDER[j]
-            prepare_group(k, (j + 2) % 4, "pa" if j % 2 == 0 else "pb")
-            if j == 2:
-                keep_busy("pb", 2)
-            if j == C_LAST_AFTER:
-                for fh in range(2):
-                    nc.scalar.copy(out=c_last[:, fh, :], in_=column_sum(NT - 1, fh)[:])
-                nc.sync.dma_start(out=work[1:P:2, c_at(-1, 0):c_at(-1, 0) + 2, :], in_=c_last[0:P:2, :, :])
-                for jj in range(2, j):
-                    move(ORDER[jj] * GRP, GRP, True)
-            if j >= C_LAST_AFTER:
-                move(k * GRP, GRP, True)
+        def above_below(t, fh):
+            pa = psum.tile([P, HALF], F32, tag="pa", bufs=BANKS["pa"], name="pa")
+            mx(pa, -1, t, fh, True, False)
+            mx(pa, 1, t, fh, False, True)
+            return pa
 
-        for j in range(2, NG - LATE):
-            next_group(j)
+        def add_from(acc, dst, other):
+            nc.vector.tensor_tensor(out=work[:, dst, :], in0=acc[:], in1=work[:, other, :], op=ADD)
+
+        held = []
 
         def first_part(t, fh):
             if is_direct(t, fh):
                 pb = column_sum(t, fh)
-                if t == NT - 3:
-                    nc.vector.tensor_tensor(out=work[:, c_at(t, fh), :], in0=pb[:], in1=c_last[:, fh, :], op=ADD)
-                elif t == NT - 2:
-                    nc.vector.tensor_tensor(out=work[:, c_at(t, fh), :], in0=pb[:], in1=c_right[:, fh, :], op=ADD)
-                else:
+                if t < 25:
                     nc.scalar.copy(out=work[:, c_at(t, fh), :], in_=pb[:])
-                if t > 0 and last_add(t - 1, fh) == "p":
-                    nc.vector.tensor_tensor(out=work[:, d_at(t - 1, fh), :], in0=pb[:], in1=work[:, d_at(t - 1, fh), :], op=ADD)
-            elif t < NT - 1:
-                pb = psum.tile([P, HALF], F32, tag="pb", bufs=BANKS["pb"], name="pb")
-                mx(pb, 0, t, fh, True, True)
-                nc.scalar.copy(out=work[:, b_at(t, fh), :], in_=pb[:])
+                if t == 25:
+                    nc.vector.tensor_tensor(out=work[:, c_at(t, fh), :], in0=pb[:], in1=c_right[:, fh, :], op=ADD)
+                if last_add(t - 1, fh) == "p":
+                    add_from(pb, d_at(t - 1, fh), d_at(t - 1, fh))
+                if t == 26:
+                    add_from(pb, d_at(27, fh), d_at(27, fh))
+                return
+            pb = psum.tile([P, HALF], F32, tag="pb", bufs=BANKS["pb"], name="pb")
+            mx(pb, 0, t, fh, True, True)
+            nc.scalar.copy(out=work[:, b_at(t, fh), :], in_=pb[:])
 
         def second_part(t, fh):
-            pa = psum.tile([P, HALF], F32, tag="pa", bufs=BANKS["pa"], name="pa")
-            mx(pa, -1, t, fh, True, False)
-            mx(pa, 1, t, fh, False, True)
-            if is_direct(t, fh) or t == NT - 1:
-                nc.vector.tensor_tensor(out=work[:, d_at(t, fh), :], in0=pa[:], in1=work[:, c_at(t - 1, fh), :], op=ADD)
+            pa = above_below(t, fh)
+            if t == NT - 1:
+                add_from(pa, c_at(t, fh), b_at(t, fh))
+                held.append(pa)
+            elif is_direct(t, fh):
+                add_from(pa, d_at(t, fh), c_before(t, fh))
             else:
+                d, c, before, b = d_at(t, fh), c_at(t, fh), c_before(t, fh), b_at(t, fh)
                 nc.vector.tensor_tensor(
-                    out=work[:, d_at(t, fh):c_at(t, fh) + 1:c_at(t, fh) - d_at(t, fh), :],
+                    out=work[:, d:c + 1:c - d, :],
                     in0=pa[:].unsqueeze(1).to_broadcast([P, 2, HALF]),
-                    in1=work[:, c_at(t - 1, fh):b_at(t, fh) + 1:b_at(t, fh) - c_at(t - 1, fh), :],
+                    in1=work[:, before:b + 1:b - before, :],
                     op=ADD,
                 )
 
@@ -262,9 +279,13 @@ def tile_graphconvlayer_t_kernel(tc, X, Wm, b, H, W, grad_out, out):
             halves = [fh for fh in range(2) if last_add(t, fh) == "g"]
             if halves:
                 lo = halves[0]
-                hi = halves[-1] + 1
-                dst = work[:, d_at(t, lo):d_at(t, lo) + hi - lo, :]
-                nc.gpsimd.tensor_tensor(out=dst, in0=dst, in1=work[:, c_at(t + 1, lo):c_at(t + 1, lo) + hi - lo, :], op=ADD)
+                n = halves[-1] + 1 - lo
+                dst = work[:, d_at(t, lo):d_at(t, lo) + n, :]
+                after = c_right[:] if t == NT - 1 else None
+                if after is None:
+                    c = c_at(t - 1 if t > 28 else t + 1, lo)
+                    after = work[:, c:c + n, :]
+                nc.gpsimd.tensor_tensor(out=dst, in0=dst, in1=after, op=ADD)
 
         def store(t, n):
             for q in range(4):
@@ -273,33 +294,68 @@ def tile_graphconvlayer_t_kernel(tc, X, Wm, b, H, W, grad_out, out):
                     in_=work[q:P:4, d_at(t, 0):d_at(t, 0) + 2 * n, :].rearrange("p (a v) f -> p a (v f)", v=2),
                 )
 
-        for t in range(NT):
-            if t == NT - 2:
-                first_part(t, 0)
-                first_part(t, 1)
-                store(t - 1, 1)
-                second_part(t, 0)
-                second_part(t, 1)
-            else:
-                for fh in range(2):
-                    first_part(t, fh)
-                    if t > 0:
-                        second_part(t, fh)
-                    if 2 * t + fh - 1 in range(LATE):
-                        next_group(NG - LATE + 2 * t + fh - 1)
+        keep_busy("pb", 10)
+        stage_group(0)
+        quantise_group(0)
+        keep_busy("pa", 2)
+        stage_w(0)
+        quantise_w(0)
+        keep_busy("pa", 2)
+        stage_w(1)
+        move_group(0)
+        quantise_w(1)
+        keep_busy("pa", 2)
+        for j in range(1, EARLY + 1):
+            stage_group(j)
+            quantise_group(j)
+            move_group(j)
+
+        for s in range(NT - 1):
+            t = SEQ[s]
+            for fh in range(2):
+                j = EARLY + 1 + 2 * s + fh
+                if t == 26 and fh == 1:
+                    continue
+                first_part(t, fh)
+                if t == 26:
+                    first_part(t, 1)
+                    store(25, 1)
+                    store(27, 1)
+                    second_part(t, 0)
+                    second_part(t, 1)
+                    continue
+                second_part(t, fh)
+                if j < NG:
+                    stage_group(j)
+                    quantise_group(j)
+                    move_group(j)
+                if s == 1:
+                    add_from(held[fh], d_at(NT - 1, fh), c_at(NT - 2, fh))
+            if s == 0:
+                nc.sync.dma_start(out=work[1:P:2, C_LEFT:C_LEFT + 2, :], in_=work[0:P:2, c_at(NT - 1, 0):c_at(NT - 1, 0) + 2, :])
             if t == 0:
                 nc.sync.dma_start(out=c_right[0:P:2, :, :], in_=work[1:P:2, c_at(0, 0):c_at(0, 0) + 2, :])
-            if t == 2:
-                move(NT - GRP, GRP - 1, True)
-            if t == 1:
-                second_part(0, 0)
-                second_part(0, 1)
-            if t >= 1:
+            if s == A27_AT:
+                for fh in range(2):
+                    pb = column_sum(27, fh)
+                    nc.scalar.copy(out=c_right[:, fh, :], in_=pb[:])
+                    add_from(pb, d_at(28, fh), d_at(28, fh))
+                    add_from(above_below(27, fh), d_at(27, fh), c_at(28, fh))
+                store(28, 1)
+            if s == G_FROM:
+                finish(30)
+                finish(29)
+                for tt in range(t):
+                    finish(tt)
+            elif s > G_FROM:
                 finish(t - 1)
-            if 2 <= t <= NT - GRP and t % 2 == 0:
-                store(t - 2, 2)
-            if t == NT - 3:
-                store(t - 1, 1)
-            if t == NT - 2:
-                store(t, 1)
-        store(NT - 1, 1)
+            if s == ZERO_AFTER:
+                finish(31)
+                store(29, 3)
+            if s > G_FROM and t % 2 == 0 and t < 25:
+                for tt in range(0 if s <= G_FROM + 2 else t - 2, t, 2):
+                    store(tt, 2)
+            if t == 25:
+                store(24, 1)
+            if t == 26:
+                store(26, 1)

from contextlib import ExitStack

import concourse.mybir as mybir
from concourse.masks import make_identity

F32 = mybir.dt.float32
BF16 = mybir.dt.bfloat16
U32 = mybir.dt.uint32
U8 = mybir.dt.uint8
I32 = mybir.dt.int32
E5X4 = mybir.dt.float8_e5m2_x4
E4X4 = mybir.dt.float8_e4m3fn_x4
ADD = mybir.AluOpType.add

P = 128
NODES = 4096
K = 512
FEAT = 1024
HALF = 512
NT = 32
GRP = 4
NG = NT // GRP
ND = 14
NC = 6
NB = 4
STEP = 4
FLOPS = 2 * NODES * K * FEAT
BYTES = NODES * K * 2 + FEAT * K * 2 + NODES * FEAT * 4

SEQ = (31, 30, 29, 28) + tuple(range(27))
GROUPS = (7,) + tuple(range(7))
SHIFTS = (-1, 0, 1)
BANKS = {"pa": 4, "pb": 4}
EARLY = 1
G_FROM = 6
A27_AT = 16
ZERO_AFTER = 8
VMOVE = 1
VREG = (0, )


def is_direct(t, fh):
    return t in (24, 25, 26) or (fh == 1 and t < 24 and t % 3 != 0 and t % 9 != 7)


def last_add(t, fh):
    if t in (24, 25) or (t < 24 and fh == 1 and (t % 3 == 1 or t in (12, 21))) or (t == 23 and fh == 0):
        return "p"
    return "none" if t == 26 else "g"


def tile_graphconvlayer_t_kernel(tc, X, Wm, b, H, W, grad_out, out):
    nc = tc.nc
    assert H == 32 and W == 64
    g_pt = grad_out.flatten_outer_dims().rearrange("(p t) k -> p t k", t=NT)
    w_pj = Wm.rearrange("(j p) k -> p j k", p=P)
    out_q = out.rearrange("i (r h t) f -> i h r t f", h=2, t=NT)

    with ExitStack() as ctx:
        keep = ctx.enter_context(tc.tile_pool(name="keep", bufs=1))
        psum = ctx.enter_context(tc.psum_pool(name="psum", bufs=2))

        w_sb = keep.tile([P, 8 * K], BF16, name="w_sb")
        g_sb = [keep.tile([P, GRP * K], BF16, name="g_sb%d" % g) for g in range(NG)]

        def load_w(h):
            nc.sync.dma_start(
                out=w_sb[:, h * 4 * K:(h + 1) * 4 * K].rearrange("p (j k) -> p j k", k=K),
                in_=w_pj[:, h * 4:(h + 1) * 4, :],
            )

        def load_g(g):
            nc.sync.dma_start(
                out=g_sb[g][:].rearrange("p (t k) -> p t k", k=K),
                in_=g_pt[:, g * GRP:(g + 1) * GRP, :],
            )

        load_g(GROUPS[0])
        load_w(0)
        load_w(1)
        for g in GROUPS[1:]:
            load_g(g)

        ctx.enter_context(tc.manual_schedule())

        zeros = keep.tile([P, HALF], BF16, name="zeros")
        nc.vector.memset(zeros[:], 0.0)

        def keep_busy(tag, n):
            idle = psum.tile([P, HALF], F32, tag=tag, bufs=BANKS[tag], name="idle")
            for i in range(n):
                nc.tensor.matmul(idle[:], lhsT=zeros[:, 0:P], rhs=zeros[:], start=True, stop=True)

        ident = keep.tile([P, P], F32, name="ident")
        make_identity(nc, ident[:])
        perm = keep.tile([P, P], F32, name="perm")
        nc.vector.tensor_copy(
            out=perm[:].rearrange("p (r i h) -> p r i h", i=2, h=2),
            in_=ident[:].rearrange("p (i r h) -> p r i h", i=2, h=2),
        )
        codes = {}
        scales = {}
        for s in SHIFTS:
            codes[s] = keep.tile([P, NT * P], U32, name="codes%d" % (s + 1), align_bytes=64)
            scales[s] = keep.tile([P, NT * P], U8, name="scales%d" % (s + 1), align_bytes=64)
            nc.vector.memset(scales[s][:].bitcast(I32), 0)
        nc.vector.memset(codes[1][:].bitcast(I32).rearrange("p (a c) -> p a c", c=P)[:, :, P - STEP:P], 0)
        nc.vector.memset(codes[-1][:].bitcast(I32).rearrange("p (a c) -> p a c", c=P)[:, :, 0:STEP], 0)

        stage = keep.tile([P, 4 * GRP * P * 4], BF16, name="stage", align_bytes=64)
        w_codes = keep.tile([P, FEAT], U32, name="w_codes", align_bytes=64)
        w_scales = keep.tile([P, FEAT], U8, name="w_scales", align_bytes=64)
        c_right = keep.tile([P, 2, HALF], F32, name="c_right")
        work = keep.tile([P, 2 * (ND + NC + NB + 2), HALF], F32, name="work")
        D_28 = 2 * (ND + NC + NB)
        C_28 = D_28 + 2

        def d_at(t, fh):
            if t == 28:
                return D_28 + fh
            if t == 27:
                return C_28 + fh
            return 2 * ((t + 4 if t < 27 else t - 28) % ND) + fh

        def c_ring(s, fh):
            return 2 * ND + 2 * (s % NC) + fh

        def c_at(t, fh):
            return C_28 + fh if t == 28 else c_ring(SEQ.index(t), fh)

        def c_before(t, fh):
            return c_ring(SEQ.index(t) - 1, fh)

        def b_at(t, fh):
            return 2 * (ND + NC) + 2 * (SEQ.index(t) % NB) + fh

        C_LEFT = c_ring(3, 0)
        nc.gpsimd.memset(work[:, C_LEFT:C_LEFT + 2, :], 0.0)
        nc.gpsimd.memset(c_right[:], 0.0)

        def transposes(tag, src32, first, mat):
            xt = psum.tile([P, 2, 256], F32, tag=tag, bufs=BANKS[tag], name="xt")
            for jj in range(2):
                for u in range(2):
                    lo = (first + jj) * 256 + u * P
                    nc.tensor.transpose(xt[:, u, jj * P:(jj + 1) * P], src32[:, lo:lo + P], mat[:])
            return xt

        def regroup(engine, xt, word0):
            engine(
                out=stage[:].bitcast(F32)[:, word0:word0 + 512].rearrange("p (n u) -> p n u", u=2),
                in_=xt[:].rearrange("p u n -> p n u"),
            )

        def stage_in(src, first, buf, tag, mat, second_engine):
            src32 = src[:].bitcast(F32)
            xt = [transposes(tag, src32, first, mat), transposes(tag, src32, first + 2, mat)]
            regroup(nc.scalar.copy, xt[0], buf * 1024)
            regroup(second_engine, xt[1], buf * 1024 + 512)

        def move(slot0, ntile, by_dma, scale_engine=None):
            lo = slot0 * P
            hi = (slot0 + ntile) * P
            mid = codes[0][:].bitcast(I32)[:, lo:hi].rearrange("p (a c) -> p a c", c=P)
            up = codes[1][:].bitcast(I32)[:, lo:hi].rearrange("p (a c) -> p a c", c=P)
            dn = codes[-1][:].bitcast(I32)[:, lo:hi].rearrange("p (a c) -> p a c", c=P)
            wlo = lo // 4
            whi = hi // 4
            smid = scales[0][:].bitcast(I32)
            pairs = [
                (up[:, :, 0:P - STEP], mid[:, :, STEP:P]),
                (dn[:, :, STEP:P], mid[:, :, 0:P - STEP]),
                (scales[1][:].bitcast(I32)[:, wlo:whi - 1], smid[:, wlo + 1:whi]),
                (scales[-1][:].bitcast(I32)[:, wlo + 1:whi], smid[:, wlo:whi - 1]),
            ]
            for dst, src in pairs:
                if by_dma:
                    nc.sync.dma_start(out=dst, in_=src)
                elif scale_engine is not None and len(dst.shape) == 2:
                    scale_engine.tensor_copy(out=dst, in_=src)
                else:
                    nc.vector.tensor_copy(out=dst, in_=src)

        def stage_group(j):
            stage_in(g_sb[GROUPS[j]], 0, j % 4, "pb", perm, nc.vector.tensor_copy if j in VREG else nc.scalar.copy)

        def quantise_group(j):
            buf = j % 4
            k = GROUPS[j]
            nc.vector.quantize_mx(
                out=codes[0][:, k * GRP * P:(k + 1) * GRP * P].bitcast(E5X4),
                scales=scales[0][:, k * GRP * P:(k + 1) * GRP * P],
                in_=stage[:, buf * 2048:(buf + 1) * 2048],
            )

        def move_group(j):
            k = GROUPS[j]
            if j == NG - 1:
                move(k * GRP + 3, 1, False, nc.gpsimd)
                move(k * GRP, GRP - 1, True)
            elif j < VMOVE:
                move(k * GRP, GRP, False)
            else:
                move(k * GRP, GRP, True)

        def stage_w(h):
            stage_in(w_sb, 4 * h, 2 + h, "pa", ident, nc.scalar.copy)

        def quantise_w(h):
            buf = 2 + h
            nc.vector.quantize_mx(
                out=w_codes[:, h * 512:(h + 1) * 512].bitcast(E4X4),
                scales=w_scales[:, h * 512:(h + 1) * 512],
                in_=stage[:, buf * 2048:(buf + 1) * 2048],
            )

        def mx(acc, s, t, fh, start, stop):
            nc.tensor.matmul_mx(
                out=acc[:],
                lhsT=codes[s][:, t * P:(t + 1) * P].bitcast(E5X4),
                lhsT_scale=scales[s][:, t * P:(t + 1) * P],
                rhs=w_codes[:, fh * 512:(fh + 1) * 512].bitcast(E4X4),
                rhs_scale=w_scales[:, fh * 512:(fh + 1) * 512],
                start=start,
                stop=stop,
            )

        def column_sum(t, fh):
            pb = psum.tile([P, HALF], F32, tag="pb", bufs=BANKS["pb"], name="pb")
            mx(pb, -1, t, fh, True, False)
            mx(pb, 0, t, fh, False, False)
            mx(pb, 1, t, fh, False, True)
            return pb

        def above_below(t, fh):
            pa = psum.tile([P, HALF], F32, tag="pa", bufs=BANKS["pa"], name="pa")
            mx(pa, -1, t, fh, True, False)
            mx(pa, 1, t, fh, False, True)
            return pa

        def add_from(acc, dst, other):
            nc.vector.tensor_tensor(out=work[:, dst, :], in0=acc[:], in1=work[:, other, :], op=ADD)

        held = []

        def first_part(t, fh):
            if is_direct(t, fh):
                pb = column_sum(t, fh)
                if t < 25:
                    nc.scalar.copy(out=work[:, c_at(t, fh), :], in_=pb[:])
                if t == 25:
                    nc.vector.tensor_tensor(out=work[:, c_at(t, fh), :], in0=pb[:], in1=c_right[:, fh, :], op=ADD)
                if last_add(t - 1, fh) == "p":
                    add_from(pb, d_at(t - 1, fh), d_at(t - 1, fh))
                if t == 26:
                    add_from(pb, d_at(27, fh), d_at(27, fh))
                return
            pb = psum.tile([P, HALF], F32, tag="pb", bufs=BANKS["pb"], name="pb")
            mx(pb, 0, t, fh, True, True)
            nc.scalar.copy(out=work[:, b_at(t, fh), :], in_=pb[:])

        def second_part(t, fh):
            pa = above_below(t, fh)
            if t == NT - 1:
                add_from(pa, c_at(t, fh), b_at(t, fh))
                held.append(pa)
            elif is_direct(t, fh):
                add_from(pa, d_at(t, fh), c_before(t, fh))
            else:
                d, c, before, b = d_at(t, fh), c_at(t, fh), c_before(t, fh), b_at(t, fh)
                nc.vector.tensor_tensor(
                    out=work[:, d:c + 1:c - d, :],
                    in0=pa[:].unsqueeze(1).to_broadcast([P, 2, HALF]),
                    in1=work[:, before:b + 1:b - before, :],
                    op=ADD,
                )

        def finish(t):
            halves = [fh for fh in range(2) if last_add(t, fh) == "g"]
            if halves:
                lo = halves[0]
                n = halves[-1] + 1 - lo
                dst = work[:, d_at(t, lo):d_at(t, lo) + n, :]
                after = c_right[:] if t == NT - 1 else None
                if after is None:
                    c = c_at(t - 1 if t > 28 else t + 1, lo)
                    after = work[:, c:c + n, :]
                nc.gpsimd.tensor_tensor(out=dst, in0=dst, in1=after, op=ADD)

        def store(t, n):
            for q in range(4):
                nc.sync.dma_start(
                    out=out_q[q // 2, q % 2, :, t:t + n, :],
                    in_=work[q:P:4, d_at(t, 0):d_at(t, 0) + 2 * n, :].rearrange("p (a v) f -> p a (v f)", v=2),
                )

        keep_busy("pb", 10)
        stage_group(0)
        quantise_group(0)
        keep_busy("pa", 2)
        stage_w(0)
        quantise_w(0)
        keep_busy("pa", 2)
        stage_w(1)
        move_group(0)
        quantise_w(1)
        keep_busy("pa", 2)
        for j in range(1, EARLY + 1):
            stage_group(j)
            quantise_group(j)
            move_group(j)

        for s in range(NT - 1):
            t = SEQ[s]
            for fh in range(2):
                j = EARLY + 1 + 2 * s + fh
                if t == 26 and fh == 1:
                    continue
                first_part(t, fh)
                if t == 26:
                    first_part(t, 1)
                    store(25, 1)
                    store(27, 1)
                    second_part(t, 0)
                    second_part(t, 1)
                    continue
                second_part(t, fh)
                if j < NG:
                    stage_group(j)
                    quantise_group(j)
                    move_group(j)
                if s == 1:
                    add_from(held[fh], d_at(NT - 1, fh), c_at(NT - 2, fh))
            if s == 0:
                nc.sync.dma_start(out=work[1:P:2, C_LEFT:C_LEFT + 2, :], in_=work[0:P:2, c_at(NT - 1, 0):c_at(NT - 1, 0) + 2, :])
            if t == 0:
                nc.sync.dma_start(out=c_right[0:P:2, :, :], in_=work[1:P:2, c_at(0, 0):c_at(0, 0) + 2, :])
            if s == A27_AT:
                for fh in range(2):
                    pb = column_sum(27, fh)
                    nc.scalar.copy(out=c_right[:, fh, :], in_=pb[:])
                    add_from(pb, d_at(28, fh), d_at(28, fh))
                    add_from(above_below(27, fh), d_at(27, fh), c_at(28, fh))
                store(28, 1)
            if s == G_FROM:
                finish(30)
                finish(29)
                for tt in range(t):
                    finish(tt)
            elif s > G_FROM:
                finish(t - 1)
            if s == ZERO_AFTER:
                finish(31)
                store(29, 3)
            if s > G_FROM and t % 2 == 0 and t < 25:
                for tt in range(0 if s <= G_FROM + 2 else t - 2, t, 2):
                    store(tt, 2)
            if t == 25:
                store(24, 1)
            if t == 26:
                store(26, 1)
